import numpy as np
import ml_dtypes


def mxq(x, axis, fmt="e4m3"):
    dtype, down = {"e4m3": (ml_dtypes.float8_e4m3fn, 7), "e5m2": (ml_dtypes.float8_e5m2, 14)}[fmt]
    v = np.moveaxis(np.asarray(x, np.float32).astype(ml_dtypes.bfloat16).astype(np.float64), axis, -1)
    blocks = v.reshape(v.shape[:-1] + (-1, 32))
    amax = np.abs(blocks).max(-1, keepdims=True)
    byte = np.maximum(np.where(amax > 0, np.frexp(amax)[1] - 1 + 127, 0) - down, 1)
    scale = np.exp2(byte - 127.0)
    codes = (blocks / scale).astype(np.float32).astype(dtype).astype(np.float64)
    return np.moveaxis((codes * scale).reshape(v.shape), -1, axis)


WIDE = False


def mx_kscale(k):
    if not WIDE:
        return np.ones(k)
    levels = np.array([20, -20, 10, -10, 0])
    a = np.random.permutation(np.resize(levels, k // 512 * 4)).reshape(k // 512, 4)
    idx = np.arange(k)
    return np.exp2(a[idx // 512, idx % 128 // 32])


BF16 = ml_dtypes.bfloat16


def bf(x):
    return np.asarray(x, np.float32).astype(BF16)


def f64(x):
    return np.asarray(x).astype(np.float64)


B, D, U = 512, 1024, 512
KD = 3 * U + D
G = 4 * U


def gate_probs(x, left_state, top_state, diagonal_state, w_zi, b_zi, w_zl, b_zl, w_zt, b_zt, w_zd, b_zd):
    q = np.concatenate([f64(left_state), f64(top_state), f64(diagonal_state), f64(x)], axis=1)
    W = np.concatenate([f64(w_zi), f64(w_zl), f64(w_zt), f64(w_zd)], axis=1)
    b = np.concatenate([f64(b_zi), f64(b_zl), f64(b_zt), f64(b_zd)])
    g = (q @ W + b).reshape(-1, 4, U)
    e = np.exp(g - g.max(axis=1, keepdims=True))
    return e / e.sum(axis=1, keepdims=True)


def setup_inputs():
    t = np.sort(mx_kscale(G))[::4]

    def gate():
        return bf(np.random.standard_normal((KD, U)) * 1.25 / np.sqrt(KD))

    def bias():
        return bf(np.random.standard_normal(U) * 0.5)

    x = bf(np.random.standard_normal((B, D)))
    left = bf(np.random.standard_normal((B, U)))
    top = bf(np.random.standard_normal((B, U)))
    diag = bf(np.random.standard_normal((B, U)))
    h_cand = bf(np.tanh(np.random.standard_normal((B, U))))
    w_zi0 = gate()
    b_zi = bias()
    w_zl0 = gate()
    b_zl = bias()
    w_zt0 = gate()
    b_zt = bias()
    w_zd0 = gate()
    b_zd = bias()
    g = bf(np.random.standard_normal((B, U)) * np.exp2(np.random.randint(-12, 1, (B, 1))) * 256.0 * t)
    z = gate_probs(x, left, top, diag, w_zi0, b_zi, w_zl0, b_zl, w_zt0, b_zt, w_zd0, b_zd).reshape(B, G)
    return {"x": x, "left_state": left, "top_state": top, "diagonal_state": diag, "h_cand": h_cand,
            "w_zi": bf(f64(w_zi0) / t), "b_zi": b_zi, "w_zl": bf(f64(w_zl0) / t), "b_zl": b_zl,
            "w_zt": bf(f64(w_zt0) / t), "b_zt": b_zt, "w_zd": bf(f64(w_zd0) / t), "b_zd": b_zd,
            "z": np.asarray(z, np.float32), "grad_out": g}


def reference(x, left_state, top_state, diagonal_state, h_cand, w_zi, b_zi, w_zl, b_zl, w_zt, b_zt, w_zd, b_zd, z, grad_out):
    zf = f64(z).reshape(-1, 4, U)
    v = np.stack([f64(h_cand), f64(left_state), f64(top_state), f64(diagonal_state)], axis=1)
    h = (zf * v).sum(axis=1, keepdims=True)
    dg = (f64(grad_out)[:, None, :] * zf * (v - h)).reshape(-1, G)
    Wx = np.concatenate([f64(w_zi)[3 * U:], f64(w_zl)[3 * U:], f64(w_zt)[3 * U:], f64(w_zd)[3 * U:]], axis=1)
    return mxq(dg, 1, "e5m2") @ mxq(Wx, 1, "e4m3").T

@@ -1,0 +1,194 @@
+from contextlib import ExitStack
+
+import concourse.mybir as mybir
+from concourse.masks import make_identity
+
+F32 = mybir.dt.float32
+BF16 = mybir.dt.bfloat16
+U32 = mybir.dt.uint32
+U8 = mybir.dt.uint8
+E4M3_X4 = mybir.dt.float8_e4m3fn_x4
+E5M2_X4 = mybir.dt.float8_e5m2_x4
+ADD = mybir.AluOpType.add
+SUB = mybir.AluOpType.subtract
+MULT = mybir.AluOpType.mult
+
+P = 128
+PACK = 4
+B, D, U = 512, 1024, 512
+GATES = 4
+KD = 3 * U + D
+B_TILES = B // P
+D_TILES = D // P
+N_MOVE = 512
+D_HALVES = D // N_MOVE
+
+FLOPS = 2 * B * D * GATES * U
+BYTES = 4 * B * GATES * U + 2 * 5 * B * U + 2 * GATES * D * U + 4 * B * D
+
+
+def tile_multidimensinalgrucell_pb_v_kernel(
+    tc,
+    x,
+    left_state,
+    top_state,
+    diagonal_state,
+    h_cand,
+    w_zi,
+    b_zi,
+    w_zl,
+    b_zl,
+    w_zt,
+    b_zt,
+    w_zd,
+    b_zd,
+    z,
+    grad_out,
+    out,
+):
+    nc = tc.nc
+    blended = [h_cand, left_state, top_state, diagonal_state]
+    weights = [w_zi, w_zl, w_zt, w_zd]
+
+    z_rows = z.rearrange("(p t) (g u) -> p t g u", t=B_TILES, g=GATES)
+    blended_rows = [v.rearrange("(p t) u -> p t u", t=B_TILES) for v in blended]
+    grad_rows = grad_out.rearrange("(p t) u -> p t u", t=B_TILES)
+    out_rows = out.rearrange("(p t) d -> p t d", t=B_TILES)
+
+    with ExitStack() as ctx:
+        inputs = ctx.enter_context(tc.tile_pool(name="inputs", bufs=1))
+        keep = ctx.enter_context(tc.tile_pool(name="keep", bufs=1))
+        work = ctx.enter_context(tc.tile_pool(name="work", bufs=2))
+        psum = ctx.enter_context(tc.psum_pool(name="psum", bufs=2))
+
+        z_tiles, v_tiles, grad_tiles, w_tiles = [], [], [], []
+
+        def load_batch_tile(bt):
+            z_t = inputs.tile([P, GATES, U], F32, name="z%d" % bt)
+            v_t = inputs.tile([P, GATES, U], BF16, name="v%d" % bt)
+            grad_t = inputs.tile([P, U], BF16, name="grad%d" % bt)
+            nc.sync.dma_start(out=z_t[:], in_=z_rows[:, bt, :, :])
+            for g in range(GATES):
+                nc.sync.dma_start(out=v_t[:, g, :], in_=blended_rows[g][:, bt, :])
+            nc.sync.dma_start(out=grad_t[:], in_=grad_rows[:, bt, :])
+            z_tiles.append(z_t)
+            v_tiles.append(v_t)
+            grad_tiles.append(grad_t)
+
+        def load_weight(g):
+            w_t = inputs.tile([P, D_TILES, U], BF16, name="w%d" % g)
+            nc.sync.dma_start(
+                out=w_t[:], in_=weights[g][KD - D : KD, :].rearrange("(t p) u -> p t u", p=P)
+            )
+            w_tiles.append(w_t)
+
+        load_batch_tile(0)
+        load_batch_tile(1)
+        for g in range(GATES):
+            load_weight(g)
+        load_batch_tile(2)
+        load_batch_tile(3)
+
+        identity = keep.tile([P, P], F32, name="identity")
+        make_identity(nc, identity[:])
+
+        w_codes = keep.tile([P, GATES, D], U32, name="w_codes", align_bytes=64)
+        w_scales = keep.tile([P, GATES, D], U8, name="w_scales", align_bytes=64)
+        dg_codes = keep.tile([P, B_TILES, GATES, P], U32, name="dg_codes", align_bytes=64)
+        dg_scales = keep.tile([P, B_TILES, GATES, P], U8, name="dg_scales", align_bytes=64)
+
+        def quantise_weight(g):
+            words = w_tiles[g][:].bitcast(F32).rearrange("p t (q c) -> p t c q", c=2)
+            grouped = work.tile([P, D, PACK], BF16, tag="w_grouped", align_bytes=64)
+            grouped_words = grouped[:].bitcast(F32)
+            for pair in range(D_TILES // 2):
+                turned = psum.tile([P, 2, 2 * P], F32, tag="w_turned")
+                for j in range(2):
+                    for c in range(2):
+                        nc.tensor.transpose(
+                            turned[:, c, j * P : (j + 1) * P], words[:, 2 * pair + j, c, :], identity[:]
+                        )
+                nc.scalar.copy(
+                    out=grouped_words[:, 2 * pair * P : (2 * pair + 2) * P, :],
+                    in_=turned[:].rearrange("q c d -> q d c"),
+                )
+            nc.vector.quantize_mx(
+                out=w_codes[:, g, :].bitcast(E4M3_X4),
+                scales=w_scales[:, g, :],
+                in_=grouped[:].rearrange("q d t -> q (d t)"),
+            )
+
+        def softmax_backward(bt):
+            z_t, v_t, grad_t = z_tiles[bt], v_tiles[bt], grad_tiles[bt]
+            prod = work.tile([P, GATES, U], F32, tag="prod")
+            pair_sum = work.tile([P, 2, U], F32, tag="pair_sum")
+            h = work.tile([P, U], F32, tag="h")
+            dg = work.tile([P, GATES, U], F32, tag="dg")
+            halves = [slice(0, U // 2), slice(U // 2, U)]
+            for cols in halves:
+                nc.vector.tensor_tensor(out=prod[:, :, cols], in0=z_t[:, :, cols], in1=v_t[:, :, cols], op=MULT)
+            for cols in halves:
+                nc.vector.tensor_tensor(
+                    out=pair_sum[:, :, cols], in0=prod[:, 0:2, cols], in1=prod[:, 2:4, cols], op=ADD
+                )
+            for cols in halves:
+                nc.vector.tensor_tensor(out=h[:, cols], in0=pair_sum[:, 0, cols], in1=pair_sum[:, 1, cols], op=ADD)
+            for cols in halves:
+                nc.vector.tensor_tensor(
+                    out=dg[:, :, cols],
+                    in0=v_t[:, :, cols],
+                    in1=h[:, cols].unsqueeze(1).to_broadcast([P, GATES, U // 2]),
+                    op=SUB,
+                )
+            for cols in halves:
+                nc.vector.tensor_tensor(out=dg[:, :, cols], in0=dg[:, :, cols], in1=z_t[:, :, cols], op=MULT)
+            for cols in halves:
+                nc.vector.tensor_tensor(
+                    out=dg[:, :, cols],
+                    in0=dg[:, :, cols],
+                    in1=grad_t[:, cols].unsqueeze(1).to_broadcast([P, GATES, U // 2]),
+                    op=MULT,
+                )
+            return dg
+
+        def quantise_dg(bt, dg):
+            grouped = work.tile([P, GATES, P, PACK], BF16, tag="dg_grouped", align_bytes=64)
+            for g in range(GATES):
+                planes = dg[:, g, :].rearrange("p (q t) -> p t q", t=PACK)
+                turned = psum.tile([P, PACK, P], F32, tag="dg_turned")
+                for t in range(PACK):
+                    nc.tensor.transpose(turned[:, t, :], planes[:, t, :], identity[:])
+                nc.scalar.copy(out=grouped[:, g, :, :], in_=turned[:].rearrange("q t b -> q b t"))
+            nc.vector.quantize_mx(
+                out=dg_codes[:, bt, :, :].rearrange("q g b -> q (g b)").bitcast(E5M2_X4),
+                scales=dg_scales[:, bt, :, :].rearrange("q g b -> q (g b)"),
+                in_=grouped[:].rearrange("q g b t -> q (g b t)"),
+            )
+
+        def multiply_and_store(bt):
+            result = work.tile([P, D], F32, tag="result")
+            for dh in range(D_HALVES):
+                d_cols = slice(dh * N_MOVE, (dh + 1) * N_MOVE)
+                acc = psum.tile([P, N_MOVE], F32, tag="acc")
+                for g in range(GATES):
+                    nc.tensor.matmul_mx(
+                        out=acc[:],
+                        lhsT=dg_codes[:, bt, g, :].bitcast(E5M2_X4),
+                        lhsT_scale=dg_scales[:, bt, g, :],
+                        rhs=w_codes[:, g, d_cols].bitcast(E4M3_X4),
+                        rhs_scale=w_scales[:, g, d_cols],
+                        start=(g == 0),
+                        stop=(g == GATES - 1),
+                    )
+                nc.scalar.copy(out=result[:, d_cols], in_=acc[:])
+            nc.sync.dma_start(out=out_rows[:, bt, :], in_=result[:])
+
+        dg0 = softmax_backward(0)
+        quantise_dg(0, dg0)
+        for g in range(GATES):
+            quantise_weight(g)
+        multiply_and_store(0)
+        for bt in range(1, B_TILES):
+            dg_bt = softmax_backward(bt)
+            quantise_dg(bt, dg_bt)
+            multiply_and_store(bt)

@@ -56,10 +56,13 @@ def tile_multidimensinalgrucell_pb_v_kernel(
     out_rows = out.rearrange("(p t) d -> p t d", t=B_TILES)
 
     with ExitStack() as ctx:
+        ctx.enter_context(tc.manual_schedule())
         inputs = ctx.enter_context(tc.tile_pool(name="inputs", bufs=1))
         keep = ctx.enter_context(tc.tile_pool(name="keep", bufs=1))
         work = ctx.enter_context(tc.tile_pool(name="work", bufs=2))
         psum = ctx.enter_context(tc.psum_pool(name="psum", bufs=2))
+
+        gate_pairs = [(0, 2), (2, 4)]
 
         z_tiles, v_tiles, grad_tiles, w_tiles = [], [], [], []
 
@@ -67,9 +70,10 @@ def tile_multidimensinalgrucell_pb_v_kernel(
             z_t = inputs.tile([P, GATES, U], F32, name="z%d" % bt)
             v_t = inputs.tile([P, GATES, U], BF16, name="v%d" % bt)
             grad_t = inputs.tile([P, U], BF16, name="grad%d" % bt)
-            nc.sync.dma_start(out=z_t[:], in_=z_rows[:, bt, :, :])
-            for g in range(GATES):
-                nc.sync.dma_start(out=v_t[:, g, :], in_=blended_rows[g][:, bt, :])
+            for lo, hi in gate_pairs:
+                for g in range(lo, hi):
+                    nc.sync.dma_start(out=v_t[:, g, :], in_=blended_rows[g][:, bt, :])
+                nc.sync.dma_start(out=z_t[:, lo:hi, :], in_=z_rows[:, bt, lo:hi, :])
             nc.sync.dma_start(out=grad_t[:], in_=grad_rows[:, bt, :])
             z_tiles.append(z_t)
             v_tiles.append(v_t)
@@ -83,11 +87,10 @@ def tile_multidimensinalgrucell_pb_v_kernel(
             w_tiles.append(w_t)
 
         load_batch_tile(0)
-        load_batch_tile(1)
         for g in range(GATES):
             load_weight(g)
-        load_batch_tile(2)
-        load_batch_tile(3)
+        for bt in range(1, B_TILES):
+            load_batch_tile(bt)
 
         identity = keep.tile([P, P], F32, name="identity")
         make_identity(nc, identity[:])
@@ -96,83 +99,87 @@ def tile_multidimensinalgrucell_pb_v_kernel(
         w_scales = keep.tile([P, GATES, D], U8, name="w_scales", align_bytes=64)
         dg_codes = keep.tile([P, B_TILES, GATES, P], U32, name="dg_codes", align_bytes=64)
         dg_scales = keep.tile([P, B_TILES, GATES, P], U8, name="dg_scales", align_bytes=64)
+        w_grouped = [
+            keep.tile([P, D, PACK], BF16, name="w_grouped%d" % g, align_bytes=64) for g in range(GATES)
+        ]
+        dg_grouped = [
+            keep.tile([P, GATES, P, PACK], BF16, name="dg_grouped%d" % (i), align_bytes=64) for i in range(2)
+        ]
 
-        def quantise_weight(g):
+        def turn_weight(g):
             words = w_tiles[g][:].bitcast(F32).rearrange("p t (q c) -> p t c q", c=2)
-            grouped = work.tile([P, D, PACK], BF16, tag="w_grouped", align_bytes=64)
-            grouped_words = grouped[:].bitcast(F32)
-            for pair in range(D_TILES // 2):
-                turned = psum.tile([P, 2, 2 * P], F32, tag="w_turned")
+            grouped_words = w_grouped[g][:].bitcast(F32)
+            for two in range(D_TILES // 2):
+                turned = psum.tile([P, 2, 2 * P], F32, tag="w_turned", bufs=3)
                 for j in range(2):
                     for c in range(2):
                         nc.tensor.transpose(
-                            turned[:, c, j * P : (j + 1) * P], words[:, 2 * pair + j, c, :], identity[:]
+                            turned[:, c, j * P : (j + 1) * P], words[:, 2 * two + j, c, :], identity[:]
                         )
                 nc.scalar.copy(
-                    out=grouped_words[:, 2 * pair * P : (2 * pair + 2) * P, :],
+                    out=grouped_words[:, 2 * two * P : (2 * two + 2) * P, :],
                     in_=turned[:].rearrange("q c d -> q d c"),
                 )
+
+        def quantise_weight(g):
             nc.vector.quantize_mx(
                 out=w_codes[:, g, :].bitcast(E4M3_X4),
                 scales=w_scales[:, g, :],
-                in_=grouped[:].rearrange("q d t -> q (d t)"),
+                in_=w_grouped[g][:].rearrange("q d t -> q (d t)"),
             )
 
-        def softmax_backward(bt):
-            z_t, v_t, grad_t = z_tiles[bt], v_tiles[bt], grad_tiles[bt]
+        def products(bt):
+            z_t, v_t = z_tiles[bt], v_tiles[bt]
             prod = work.tile([P, GATES, U], F32, tag="prod")
-            pair_sum = work.tile([P, 2, U], F32, tag="pair_sum")
+            part = work.tile([P, 2, U], F32, tag="part")
+            for lo, hi in gate_pairs:
+                nc.vector.tensor_tensor(out=prod[:, lo:hi, :], in0=z_t[:, lo:hi, :], in1=v_t[:, lo:hi, :], op=MULT)
+            for i in range(2):
+                nc.vector.tensor_tensor(out=part[:, i, :], in0=prod[:, 2 * i, :], in1=prod[:, 2 * i + 1, :], op=ADD)
+            return part
+
+        def blend(part):
             h = work.tile([P, U], F32, tag="h")
+            nc.vector.tensor_tensor(out=h[:], in0=part[:, 0, :], in1=part[:, 1, :], op=ADD)
+            return h
+
+        def gate_gradients(bt, h):
+            z_t, v_t, grad_t = z_tiles[bt], v_tiles[bt], grad_tiles[bt]
             dg = work.tile([P, GATES, U], F32, tag="dg")
-            halves = [slice(0, U // 2), slice(U // 2, U)]
-            for cols in halves:
-                nc.vector.tensor_tensor(out=prod[:, :, cols], in0=z_t[:, :, cols], in1=v_t[:, :, cols], op=MULT)
-            for cols in halves:
+            for lo, hi in gate_pairs:
                 nc.vector.tensor_tensor(
-                    out=pair_sum[:, :, cols], in0=prod[:, 0:2, cols], in1=prod[:, 2:4, cols], op=ADD
+                    out=dg[:, lo:hi, :], in0=v_t[:, lo:hi, :], in1=h[:].unsqueeze(1).to_broadcast([P, 2, U]), op=SUB
                 )
-            for cols in halves:
-                nc.vector.tensor_tensor(out=h[:, cols], in0=pair_sum[:, 0, cols], in1=pair_sum[:, 1, cols], op=ADD)
-            for cols in halves:
+            for lo, hi in gate_pairs:
+                nc.vector.tensor_tensor(out=dg[:, lo:hi, :], in0=dg[:, lo:hi, :], in1=z_t[:, lo:hi, :], op=MULT)
+            for lo, hi in gate_pairs:
                 nc.vector.tensor_tensor(
-                    out=dg[:, :, cols],
-                    in0=v_t[:, :, cols],
-                    in1=h[:, cols].unsqueeze(1).to_broadcast([P, GATES, U // 2]),
-                    op=SUB,
-                )
-            for cols in halves:
-                nc.vector.tensor_tensor(out=dg[:, :, cols], in0=dg[:, :, cols], in1=z_t[:, :, cols], op=MULT)
-            for cols in halves:
-                nc.vector.tensor_tensor(
-                    out=dg[:, :, cols],
-                    in0=dg[:, :, cols],
-                    in1=grad_t[:, cols].unsqueeze(1).to_broadcast([P, GATES, U // 2]),
+                    out=dg[:, lo:hi, :],
+                    in0=dg[:, lo:hi, :],
+                    in1=grad_t[:].unsqueeze(1).to_broadcast([P, 2, U]),
                     op=MULT,
                 )
-            return dg
+                turn_dg(bt, dg, lo, hi)
 
-        def quantise_dg(bt, dg):
-            grouped = work.tile([P, GATES, P, PACK], BF16, tag="dg_grouped", align_bytes=64)
-            for g in range(GATES):
+        def turn_dg(bt, dg, lo, hi):
+            for g in range(lo, hi):
                 planes = dg[:, g, :].rearrange("p (q t) -> p t q", t=PACK)
-                turned = psum.tile([P, PACK, P], F32, tag="dg_turned")
+                turned = psum.tile([P, PACK, P], F32, tag="dg_turned", bufs=3)
                 for t in range(PACK):
                     nc.tensor.transpose(turned[:, t, :], planes[:, t, :], identity[:])
-                nc.scalar.copy(out=grouped[:, g, :, :], in_=turned[:].rearrange("q t b -> q b t"))
-            nc.vector.quantize_mx(
-                out=dg_codes[:, bt, :, :].rearrange("q g b -> q (g b)").bitcast(E5M2_X4),
-                scales=dg_scales[:, bt, :, :].rearrange("q g b -> q (g b)"),
-                in_=grouped[:].rearrange("q g b t -> q (g b t)"),
-            )
+                nc.scalar.copy(out=dg_grouped[bt % 2][:, g, :, :], in_=turned[:].rearrange("q t b -> q b t"))
 
-        def multiply_and_store(bt):
-            result = work.tile([P, D], F32, tag="result")
-            for dh in range(D_HALVES):
-                d_cols = slice(dh * N_MOVE, (dh + 1) * N_MOVE)
-                acc = psum.tile([P, N_MOVE], F32, tag="acc")
-                for g in range(GATES):
+        def quantise_and_multiply(bt, lo, hi, accs):
+            nc.vector.quantize_mx(
+                out=dg_codes[:, bt, lo:hi, :].rearrange("q g b -> q (g b)").bitcast(E5M2_X4),
+                scales=dg_scales[:, bt, lo:hi, :].rearrange("q g b -> q (g b)"),
+                in_=dg_grouped[bt % 2][:, lo:hi, :, :].rearrange("q g b t -> q (g b t)"),
+            )
+            for g in range(lo, hi):
+                for dh in range(D_HALVES):
+                    d_cols = slice(dh * N_MOVE, (dh + 1) * N_MOVE)
                     nc.tensor.matmul_mx(
-                        out=acc[:],
+                        out=accs[dh][:],
                         lhsT=dg_codes[:, bt, g, :].bitcast(E5M2_X4),
                         lhsT_scale=dg_scales[:, bt, g, :],
                         rhs=w_codes[:, g, d_cols].bitcast(E4M3_X4),
@@ -180,15 +187,31 @@ def tile_multidimensinalgrucell_pb_v_kernel(
                         start=(g == 0),
                         stop=(g == GATES - 1),
                     )
-                nc.scalar.copy(out=result[:, d_cols], in_=acc[:])
-            nc.sync.dma_start(out=out_rows[:, bt, :], in_=result[:])
 
-        dg0 = softmax_backward(0)
-        quantise_dg(0, dg0)
+        def store(bt, accs):
+            for dh in range(D_HALVES):
+                d_cols = slice(dh * N_MOVE, (dh + 1) * N_MOVE)
+                result = work.tile([P, N_MOVE], F32, tag="result", bufs=4)
+                nc.scalar.copy(out=result[:], in_=accs[dh][:])
+                nc.sync.dma_start(out=out_rows[:, bt, d_cols], in_=result[:])
+
+        def new_accs():
+            return [psum.tile([P, N_MOVE], F32, tag="acc", name="acc%d" % dh) for dh in range(D_HALVES)]
+
+        for g in range(GATES):
+            turn_weight(g)
+        gate_gradients(0, blend(products(0)))
         for g in range(GATES):
             quantise_weight(g)
-        multiply_and_store(0)
         for bt in range(1, B_TILES):
-            dg_bt = softmax_backward(bt)
-            quantise_dg(bt, dg_bt)
-            multiply_and_store(bt)
+            part = products(bt)
+            accs = new_accs()
+            quantise_and_multiply(bt - 1, 0, 2, accs)
+            h = blend(part)
+            quantise_and_multiply(bt - 1, 2, 4, accs)
+            store(bt - 1, accs)
+            gate_gradients(bt, h)
+        accs = new_accs()
+        for lo, hi in gate_pairs:
+            quantise_and_multiply(B_TILES - 1, lo, hi, accs)
+        store(B_TILES - 1, accs)

@@ -86,11 +86,10 @@ def tile_multidimensinalgrucell_pb_v_kernel(
             )
             w_tiles.append(w_t)
 
-        load_batch_tile(0)
+        for bt in range(B_TILES):
+            load_batch_tile(bt)
         for g in range(GATES):
             load_weight(g)
-        for bt in range(1, B_TILES):
-            load_batch_tile(bt)
 
         identity = keep.tile([P, P], F32, name="identity")
         make_identity(nc, identity[:])
@@ -103,14 +102,18 @@ def tile_multidimensinalgrucell_pb_v_kernel(
             keep.tile([P, D, PACK], BF16, name="w_grouped%d" % g, align_bytes=64) for g in range(GATES)
         ]
         dg_grouped = [
-            keep.tile([P, GATES, P, PACK], BF16, name="dg_grouped%d" % (i), align_bytes=64) for i in range(2)
+            keep.tile([P, GATES, P, PACK], BF16, name="dg_grouped%d" % i, align_bytes=64) for i in range(2)
         ]
+        h_tiles = [keep.tile([P, U], F32, name="h%d" % bt) for bt in range(B_TILES)]
+        v_turned = [keep.tile([P, GATES, P, PACK], BF16, name="v_turned%d" % i) for i in range(2)]
+        diff = [keep.tile([P, GATES, P, PACK], F32, name="diff%d" % i) for i in range(2)]
+        h_banks, grad_banks, z_banks = {}, {}, {}
 
         def turn_weight(g):
             words = w_tiles[g][:].bitcast(F32).rearrange("p t (q c) -> p t c q", c=2)
             grouped_words = w_grouped[g][:].bitcast(F32)
             for two in range(D_TILES // 2):
-                turned = psum.tile([P, 2, 2 * P], F32, tag="w_turned", bufs=3)
+                turned = psum.tile([P, 2, 2 * P], F32, tag="stage")
                 for j in range(2):
                     for c in range(2):
                         nc.tensor.transpose(
@@ -128,54 +131,85 @@ def tile_multidimensinalgrucell_pb_v_kernel(
                 in_=w_grouped[g][:].rearrange("q d t -> q (d t)"),
             )
 
-        def products(bt):
+        def blend(engine, bt):
             z_t, v_t = z_tiles[bt], v_tiles[bt]
             prod = work.tile([P, GATES, U], F32, tag="prod")
             part = work.tile([P, 2, U], F32, tag="part")
             for lo, hi in gate_pairs:
-                nc.vector.tensor_tensor(out=prod[:, lo:hi, :], in0=z_t[:, lo:hi, :], in1=v_t[:, lo:hi, :], op=MULT)
+                engine.tensor_tensor(out=prod[:, lo:hi, :], in0=z_t[:, lo:hi, :], in1=v_t[:, lo:hi, :], op=MULT)
             for i in range(2):
-                nc.vector.tensor_tensor(out=part[:, i, :], in0=prod[:, 2 * i, :], in1=prod[:, 2 * i + 1, :], op=ADD)
-            return part
+                engine.tensor_tensor(out=part[:, i, :], in0=prod[:, 2 * i, :], in1=prod[:, 2 * i + 1, :], op=ADD)
+            engine.tensor_tensor(out=h_tiles[bt][:], in0=part[:, 0, :], in1=part[:, 1, :], op=ADD)
 
-        def blend(part):
-            h = work.tile([P, U], F32, tag="h")
-            nc.vector.tensor_tensor(out=h[:], in0=part[:, 0, :], in1=part[:, 1, :], op=ADD)
-            return h
-
-        def gate_gradients(bt, h):
-            z_t, v_t, grad_t = z_tiles[bt], v_tiles[bt], grad_tiles[bt]
-            dg = work.tile([P, GATES, U], F32, tag="dg")
+        def turn_v(bt):
+            words = v_tiles[bt][:].bitcast(F32).rearrange("p g (q c) -> p g c q", c=2)
+            turned_words = v_turned[bt % 2][:].bitcast(F32)
             for lo, hi in gate_pairs:
+                turned = psum.tile([P, 2, 2, P], F32, tag="stage")
+                for g in range(lo, hi):
+                    for c in range(2):
+                        nc.tensor.transpose(turned[:, g - lo, c, :], words[:, g, c, :], identity[:])
+                nc.scalar.copy(out=turned_words[:, lo:hi, :, :], in_=turned[:].rearrange("q g c b -> q g b c"))
+
+        def turn_grad(bt):
+            words = grad_tiles[bt][:].bitcast(F32).rearrange("p (q c) -> p c q", c=2)
+            bank = psum.tile([P, 2, P], F32, tag="grad_bank", bufs=1)
+            for c in range(2):
+                nc.tensor.transpose(bank[:, c, :], words[:, c, :], identity[:])
+            grad_banks[bt] = bank
+
+        def turn_planes(bank, rows):
+            planes = rows.rearrange("p (q t) -> p t q", t=PACK)
+            for t in range(PACK):
+                nc.tensor.transpose(bank[:, t, :], planes[:, t, :], identity[:])
+
+        def turn_h(bt):
+            h_banks[bt] = psum.tile([P, PACK, P], F32, tag="h_bank", bufs=1, name="h_bank")
+            turn_planes(h_banks[bt], h_tiles[bt][:])
+
+        def turn_z(bt, g):
+            z_banks[(bt, g)] = psum.tile([P, PACK, P], F32, tag="z_bank", name="z_bank")
+            turn_planes(z_banks[(bt, g)], z_tiles[bt][:, g, :])
+
+        def subtract_h(bt, lo, hi):
+            for g in range(lo, hi):
                 nc.vector.tensor_tensor(
-                    out=dg[:, lo:hi, :], in0=v_t[:, lo:hi, :], in1=h[:].unsqueeze(1).to_broadcast([P, 2, U]), op=SUB
+                    out=diff[bt % 2][:, g, :, :],
+                    in0=v_turned[bt % 2][:, g, :, :],
+                    in1=h_banks[bt][:].rearrange("q t b -> q b t"),
+                    op=SUB,
                 )
-            for lo, hi in gate_pairs:
-                nc.vector.tensor_tensor(out=dg[:, lo:hi, :], in0=dg[:, lo:hi, :], in1=z_t[:, lo:hi, :], op=MULT)
-            for lo, hi in gate_pairs:
+
+        def times_z(bt, lo, hi):
+            for g in range(lo, hi):
                 nc.vector.tensor_tensor(
-                    out=dg[:, lo:hi, :],
-                    in0=dg[:, lo:hi, :],
-                    in1=grad_t[:].unsqueeze(1).to_broadcast([P, 2, U]),
+                    out=diff[bt % 2][:, g, :, :],
+                    in0=diff[bt % 2][:, g, :, :],
+                    in1=z_banks[(bt, g)][:].rearrange("q t b -> q b t"),
                     op=MULT,
                 )
-                turn_dg(bt, dg, lo, hi)
 
-        def turn_dg(bt, dg, lo, hi):
+        def times_grad(bt, lo, hi):
+            grad = grad_banks[bt][:].bitcast(BF16).rearrange("q c (b e) -> q b c e", e=2)
             for g in range(lo, hi):
-                planes = dg[:, g, :].rearrange("p (q t) -> p t q", t=PACK)
-                turned = psum.tile([P, PACK, P], F32, tag="dg_turned", bufs=3)
-                for t in range(PACK):
-                    nc.tensor.transpose(turned[:, t, :], planes[:, t, :], identity[:])
-                nc.scalar.copy(out=dg_grouped[bt % 2][:, g, :, :], in_=turned[:].rearrange("q t b -> q b t"))
+                nc.vector.tensor_tensor(
+                    out=dg_grouped[bt % 2][:, g, :, :].rearrange("q b (c e) -> q b c e", e=2),
+                    in0=diff[bt % 2][:, g, :, :].rearrange("q b (c e) -> q b c e", e=2),
+                    in1=grad,
+                    op=MULT,
+                )
 
-        def quantise_and_multiply(bt, lo, hi, accs):
-            nc.vector.quantize_mx(
-                out=dg_codes[:, bt, lo:hi, :].rearrange("q g b -> q (g b)").bitcast(E5M2_X4),
-                scales=dg_scales[:, bt, lo:hi, :].rearrange("q g b -> q (g b)"),
-                in_=dg_grouped[bt % 2][:, lo:hi, :, :].rearrange("q g b t -> q (g b t)"),
-            )
-            for g in range(lo, hi):
+        def quantise_dg(bt):
+            for lo, hi in gate_pairs:
+                nc.vector.quantize_mx(
+                    out=dg_codes[:, bt, lo:hi, :].rearrange("q g b -> q (g b)").bitcast(E5M2_X4),
+                    scales=dg_scales[:, bt, lo:hi, :].rearrange("q g b -> q (g b)"),
+                    in_=dg_grouped[bt % 2][:, lo:hi, :, :].rearrange("q g b t -> q (g b t)"),
+                )
+
+        def multiply_and_store(bt):
+            accs = [psum.tile([P, N_MOVE], F32, tag="acc", name="acc%d" % dh) for dh in range(D_HALVES)]
+            for g in range(GATES):
                 for dh in range(D_HALVES):
                     d_cols = slice(dh * N_MOVE, (dh + 1) * N_MOVE)
                     nc.tensor.matmul_mx(
@@ -187,31 +221,63 @@ def tile_multidimensinalgrucell_pb_v_kernel(
                         start=(g == 0),
                         stop=(g == GATES - 1),
                     )
-
-        def store(bt, accs):
             for dh in range(D_HALVES):
                 d_cols = slice(dh * N_MOVE, (dh + 1) * N_MOVE)
                 result = work.tile([P, N_MOVE], F32, tag="result", bufs=4)
                 nc.scalar.copy(out=result[:], in_=accs[dh][:])
                 nc.sync.dma_start(out=out_rows[:, bt, d_cols], in_=result[:])
 
-        def new_accs():
-            return [psum.tile([P, N_MOVE], F32, tag="acc", name="acc%d" % dh) for dh in range(D_HALVES)]
+        def first_half(bt):
+            subtract_h(bt, 0, 2)
+            if bt > 0:
+                quantise_dg(bt - 1)
+            if bt == B_TILES // 2:
+                for g in range(GATES):
+                    quantise_weight(g)
+            times_z(bt, 0, 2)
+            turn_z(bt, 2)
+            turn_z(bt, 3)
 
-        for g in range(GATES):
-            turn_weight(g)
-        gate_gradients(0, blend(products(0)))
-        for g in range(GATES):
-            quantise_weight(g)
-        for bt in range(1, B_TILES):
-            part = products(bt)
-            accs = new_accs()
-            quantise_and_multiply(bt - 1, 0, 2, accs)
-            h = blend(part)
-            quantise_and_multiply(bt - 1, 2, 4, accs)
-            store(bt - 1, accs)
-            gate_gradients(bt, h)
-        accs = new_accs()
-        for lo, hi in gate_pairs:
-            quantise_and_multiply(B_TILES - 1, lo, hi, accs)
-        store(B_TILES - 1, accs)
+        def second_half(bt):
+            more = bt + 1 < B_TILES
+            times_grad(bt, 0, 2)
+            subtract_h(bt, 2, 4)
+            if more:
+                turn_h(bt + 1)
+            times_z(bt, 2, 4)
+            if more:
+                turn_z(bt + 1, 0)
+                turn_z(bt + 1, 1)
+            times_grad(bt, 2, 4)
+            if more:
+                turn_grad(bt + 1)
+            if bt + 2 < B_TILES:
+                turn_v(bt + 2)
+
+        blend(nc.vector, 0)
+        turn_v(0)
+        turn_grad(0)
+        turn_z(0, 0)
+        turn_z(0, 1)
+        turn_h(0)
+        blend(nc.vector, 1)
+        turn_v(1)
+        blend(nc.gpsimd, 2)
+        blend(nc.gpsimd, 3)
+        first_half(0)
+        second_half(0)
+        turn_weight(0)
+        first_half(1)
+        turn_weight(1)
+        second_half(1)
+        turn_weight(2)
+        turn_weight(3)
+        first_half(2)
+        multiply_and_store(0)
+        second_half(2)
+        multiply_and_store(1)
+        first_half(3)
+        multiply_and_store(2)
+        second_half(3)
+        quantise_dg(3)
+        multiply_and_store(3)

@@ -86,10 +86,14 @@ def tile_multidimensinalgrucell_pb_v_kernel(
             )
             w_tiles.append(w_t)
 
-        for bt in range(B_TILES):
-            load_batch_tile(bt)
-        for g in range(GATES):
-            load_weight(g)
+        load_batch_tile(0)
+        load_batch_tile(1)
+        load_weight(0)
+        load_weight(1)
+        load_batch_tile(2)
+        load_weight(2)
+        load_weight(3)
+        load_batch_tile(3)
 
         identity = keep.tile([P, P], F32, name="identity")
         make_identity(nc, identity[:])
@@ -105,7 +109,7 @@ def tile_multidimensinalgrucell_pb_v_kernel(
             keep.tile([P, GATES, P, PACK], BF16, name="dg_grouped%d" % i, align_bytes=64) for i in range(2)
         ]
         h_tiles = [keep.tile([P, U], F32, name="h%d" % bt) for bt in range(B_TILES)]
-        v_turned = [keep.tile([P, GATES, P, PACK], BF16, name="v_turned%d" % i) for i in range(2)]
+        v_turned = [keep.tile([P, GATES, P, PACK], BF16, name="v_turned%d" % bt) for bt in range(B_TILES)]
         diff = [keep.tile([P, GATES, P, PACK], F32, name="diff%d" % i) for i in range(2)]
         h_banks, grad_banks, z_banks = {}, {}, {}
 
@@ -135,15 +139,15 @@ def tile_multidimensinalgrucell_pb_v_kernel(
             z_t, v_t = z_tiles[bt], v_tiles[bt]
             prod = work.tile([P, GATES, U], F32, tag="prod")
             part = work.tile([P, 2, U], F32, tag="part")
-            for lo, hi in gate_pairs:
-                engine.tensor_tensor(out=prod[:, lo:hi, :], in0=z_t[:, lo:hi, :], in1=v_t[:, lo:hi, :], op=MULT)
+            for g in range(GATES):
+                engine.tensor_tensor(out=prod[:, g, :], in0=z_t[:, g, :], in1=v_t[:, g, :], op=MULT)
             for i in range(2):
                 engine.tensor_tensor(out=part[:, i, :], in0=prod[:, 2 * i, :], in1=prod[:, 2 * i + 1, :], op=ADD)
             engine.tensor_tensor(out=h_tiles[bt][:], in0=part[:, 0, :], in1=part[:, 1, :], op=ADD)
 
         def turn_v(bt):
             words = v_tiles[bt][:].bitcast(F32).rearrange("p g (q c) -> p g c q", c=2)
-            turned_words = v_turned[bt % 2][:].bitcast(F32)
+            turned_words = v_turned[bt][:].bitcast(F32)
             for lo, hi in gate_pairs:
                 turned = psum.tile([P, 2, 2, P], F32, tag="stage")
                 for g in range(lo, hi):
@@ -175,7 +179,7 @@ def tile_multidimensinalgrucell_pb_v_kernel(
             for g in range(lo, hi):
                 nc.vector.tensor_tensor(
                     out=diff[bt % 2][:, g, :, :],
-                    in0=v_turned[bt % 2][:, g, :, :],
+                    in0=v_turned[bt][:, g, :, :],
                     in1=h_banks[bt][:].rearrange("q t b -> q b t"),
                     op=SUB,
                 )
@@ -199,60 +203,54 @@ def tile_multidimensinalgrucell_pb_v_kernel(
                     op=MULT,
                 )
 
-        def quantise_dg(bt):
-            for lo, hi in gate_pairs:
-                nc.vector.quantize_mx(
-                    out=dg_codes[:, bt, lo:hi, :].rearrange("q g b -> q (g b)").bitcast(E5M2_X4),
-                    scales=dg_scales[:, bt, lo:hi, :].rearrange("q g b -> q (g b)"),
-                    in_=dg_grouped[bt % 2][:, lo:hi, :, :].rearrange("q g b t -> q (g b t)"),
-                )
+        def quantise_dg(bt, lo, hi):
+            nc.vector.quantize_mx(
+                out=dg_codes[:, bt, lo:hi, :].rearrange("q g b -> q (g b)").bitcast(E5M2_X4),
+                scales=dg_scales[:, bt, lo:hi, :].rearrange("q g b -> q (g b)"),
+                in_=dg_grouped[bt % 2][:, lo:hi, :, :].rearrange("q g b t -> q (g b t)"),
+            )
 
         def multiply_and_store(bt):
             accs = [psum.tile([P, N_MOVE], F32, tag="acc", name="acc%d" % dh) for dh in range(D_HALVES)]
-            for g in range(GATES):
+            for lo, hi in gate_pairs:
                 for dh in range(D_HALVES):
                     d_cols = slice(dh * N_MOVE, (dh + 1) * N_MOVE)
-                    nc.tensor.matmul_mx(
-                        out=accs[dh][:],
-                        lhsT=dg_codes[:, bt, g, :].bitcast(E5M2_X4),
-                        lhsT_scale=dg_scales[:, bt, g, :],
-                        rhs=w_codes[:, g, d_cols].bitcast(E4M3_X4),
-                        rhs_scale=w_scales[:, g, d_cols],
-                        start=(g == 0),
-                        stop=(g == GATES - 1),
-                    )
+                    for g in range(lo, hi):
+                        nc.tensor.matmul_mx(
+                            out=accs[dh][:],
+                            lhsT=dg_codes[:, bt, g, :].bitcast(E5M2_X4),
+                            lhsT_scale=dg_scales[:, bt, g, :],
+                            rhs=w_codes[:, g, d_cols].bitcast(E4M3_X4),
+                            rhs_scale=w_scales[:, g, d_cols],
+                            start=(g == 0),
+                            stop=(g == GATES - 1),
+                        )
             for dh in range(D_HALVES):
                 d_cols = slice(dh * N_MOVE, (dh + 1) * N_MOVE)
                 result = work.tile([P, N_MOVE], F32, tag="result", bufs=4)
                 nc.scalar.copy(out=result[:], in_=accs[dh][:])
                 nc.sync.dma_start(out=out_rows[:, bt, d_cols], in_=result[:])
 
-        def first_half(bt):
+        def start(bt):
             subtract_h(bt, 0, 2)
             if bt > 0:
-                quantise_dg(bt - 1)
-            if bt == B_TILES // 2:
-                for g in range(GATES):
-                    quantise_weight(g)
+                quantise_dg(bt - 1, 0, GATES)
+
+        def first_gates(bt):
             times_z(bt, 0, 2)
             turn_z(bt, 2)
             turn_z(bt, 3)
-
-        def second_half(bt):
-            more = bt + 1 < B_TILES
             times_grad(bt, 0, 2)
             subtract_h(bt, 2, 4)
-            if more:
-                turn_h(bt + 1)
+
+        def last_gates(bt):
             times_z(bt, 2, 4)
-            if more:
+            if bt + 1 < B_TILES:
                 turn_z(bt + 1, 0)
                 turn_z(bt + 1, 1)
             times_grad(bt, 2, 4)
-            if more:
+            if bt + 1 < B_TILES:
                 turn_grad(bt + 1)
-            if bt + 2 < B_TILES:
-                turn_v(bt + 2)
 
         blend(nc.vector, 0)
         turn_v(0)
@@ -264,20 +262,32 @@ def tile_multidimensinalgrucell_pb_v_kernel(
         turn_v(1)
         blend(nc.gpsimd, 2)
         blend(nc.gpsimd, 3)
-        first_half(0)
-        second_half(0)
         turn_weight(0)
-        first_half(1)
+        start(0)
+        first_gates(0)
         turn_weight(1)
-        second_half(1)
+        turn_h(1)
+        last_gates(0)
+        turn_v(2)
+        start(1)
+        first_gates(1)
         turn_weight(2)
+        turn_h(2)
+        last_gates(1)
         turn_weight(3)
-        first_half(2)
+        turn_v(3)
+        start(2)
+        for g in range(GATES):
+            quantise_weight(g)
+        first_gates(2)
         multiply_and_store(0)
-        second_half(2)
+        turn_h(3)
+        last_gates(2)
         multiply_and_store(1)
-        first_half(3)
+        start(3)
+        first_gates(3)
+        quantise_dg(3, 0, 2)
         multiply_and_store(2)
-        second_half(3)
-        quantise_dg(3)
+        last_gates(3)
+        quantise_dg(3, 2, 4)
         multiply_and_store(3)

@@ -22,6 +22,7 @@ B_TILES = B // P
 D_TILES = D // P
 N_MOVE = 512
 D_HALVES = D // N_MOVE
+TILES_PER_HALF = N_MOVE // P
 
 FLOPS = 2 * B * D * GATES * U
 BYTES = 4 * B * GATES * U + 2 * 5 * B * U + 2 * GATES * D * U + 4 * B * D
@@ -64,36 +65,35 @@ def tile_multidimensinalgrucell_pb_v_kernel(
 
         gate_pairs = [(0, 2), (2, 4)]
 
-        z_tiles, v_tiles, grad_tiles, w_tiles = [], [], [], []
+        z_tiles = [inputs.tile([P, GATES, U], F32, name="z%d" % bt) for bt in range(B_TILES)]
+        v_tiles = [inputs.tile([P, GATES, 2, U], BF16, name="v%d" % i) for i in range(B_TILES // 2)]
+        grad_tiles = [inputs.tile([P, 2, U], BF16, name="grad%d" % i) for i in range(B_TILES // 2)]
+        w_tiles = [inputs.tile([P, D_TILES, U], BF16, name="w%d" % g) for g in range(GATES)]
 
-        def load_batch_tile(bt):
-            z_t = inputs.tile([P, GATES, U], F32, name="z%d" % bt)
-            v_t = inputs.tile([P, GATES, U], BF16, name="v%d" % bt)
-            grad_t = inputs.tile([P, U], BF16, name="grad%d" % bt)
+        def load_two_batch_tiles(i):
             for lo, hi in gate_pairs:
                 for g in range(lo, hi):
-                    nc.sync.dma_start(out=v_t[:, g, :], in_=blended_rows[g][:, bt, :])
-                nc.sync.dma_start(out=z_t[:, lo:hi, :], in_=z_rows[:, bt, lo:hi, :])
-            nc.sync.dma_start(out=grad_t[:], in_=grad_rows[:, bt, :])
-            z_tiles.append(z_t)
-            v_tiles.append(v_t)
-            grad_tiles.append(grad_t)
+                    nc.sync.dma_start(out=v_tiles[i][:, g, :, :], in_=blended_rows[g][:, 2 * i : 2 * i + 2, :])
+                nc.sync.dma_start(out=z_tiles[2 * i][:, lo:hi, :], in_=z_rows[:, 2 * i, lo:hi, :])
+            nc.sync.dma_start(out=grad_tiles[i][:], in_=grad_rows[:, 2 * i : 2 * i + 2, :])
+
+        def load_z(bt):
+            for lo, hi in gate_pairs:
+                nc.sync.dma_start(out=z_tiles[bt][:, lo:hi, :], in_=z_rows[:, bt, lo:hi, :])
 
         def load_weight(g):
-            w_t = inputs.tile([P, D_TILES, U], BF16, name="w%d" % g)
             nc.sync.dma_start(
-                out=w_t[:], in_=weights[g][KD - D : KD, :].rearrange("(t p) u -> p t u", p=P)
+                out=w_tiles[g][:], in_=weights[g][KD - D : KD, :].rearrange("(p t) u -> p t u", t=D_TILES)
             )
-            w_tiles.append(w_t)
 
-        load_batch_tile(0)
-        load_batch_tile(1)
+        load_two_batch_tiles(0)
+        load_z(1)
         load_weight(0)
         load_weight(1)
-        load_batch_tile(2)
+        load_two_batch_tiles(1)
         load_weight(2)
         load_weight(3)
-        load_batch_tile(3)
+        load_z(3)
 
         identity = keep.tile([P, P], F32, name="identity")
         make_identity(nc, identity[:])
@@ -136,7 +136,7 @@ def tile_multidimensinalgrucell_pb_v_kernel(
             )
 
         def blend(engine, bt):
-            z_t, v_t = z_tiles[bt], v_tiles[bt]
+            z_t, v_t = z_tiles[bt], v_tiles[bt // 2][:, :, bt % 2, :]
             prod = work.tile([P, GATES, U], F32, tag="prod")
             part = work.tile([P, 2, U], F32, tag="part")
             for g in range(GATES):
@@ -146,7 +146,7 @@ def tile_multidimensinalgrucell_pb_v_kernel(
             engine.tensor_tensor(out=h_tiles[bt][:], in0=part[:, 0, :], in1=part[:, 1, :], op=ADD)
 
         def turn_v(bt):
-            words = v_tiles[bt][:].bitcast(F32).rearrange("p g (q c) -> p g c q", c=2)
+            words = v_tiles[bt // 2][:].bitcast(F32)[:, :, bt % 2, :].rearrange("p g (q c) -> p g c q", c=2)
             turned_words = v_turned[bt][:].bitcast(F32)
             for lo, hi in gate_pairs:
                 turned = psum.tile([P, 2, 2, P], F32, tag="stage")
@@ -156,7 +156,7 @@ def tile_multidimensinalgrucell_pb_v_kernel(
                 nc.scalar.copy(out=turned_words[:, lo:hi, :, :], in_=turned[:].rearrange("q g c b -> q g b c"))
 
         def turn_grad(bt):
-            words = grad_tiles[bt][:].bitcast(F32).rearrange("p (q c) -> p c q", c=2)
+            words = grad_tiles[bt // 2][:].bitcast(F32)[:, bt % 2, :].rearrange("p (q c) -> p c q", c=2)
             bank = psum.tile([P, 2, P], F32, tag="grad_bank", bufs=1)
             for c in range(2):
                 nc.tensor.transpose(bank[:, c, :], words[:, c, :], identity[:])
@@ -172,7 +172,7 @@ def tile_multidimensinalgrucell_pb_v_kernel(
             turn_planes(h_banks[bt], h_tiles[bt][:])
 
         def turn_z(bt, g):
-            z_banks[(bt, g)] = psum.tile([P, PACK, P], F32, tag="z_bank", name="z_bank")
+            z_banks[(bt, g)] = psum.tile([P, PACK, P], F32, tag="z_bank", bufs=GATES, name="z_bank")
             turn_planes(z_banks[(bt, g)], z_tiles[bt][:, g, :])
 
         def subtract_h(bt, lo, hi):
@@ -211,7 +211,7 @@ def tile_multidimensinalgrucell_pb_v_kernel(
             )
 
         def multiply_and_store(bt):
-            accs = [psum.tile([P, N_MOVE], F32, tag="acc", name="acc%d" % dh) for dh in range(D_HALVES)]
+            accs = [psum.tile([P, N_MOVE], F32, tag="stage", name="acc%d" % dh) for dh in range(D_HALVES)]
             for lo, hi in gate_pairs:
                 for dh in range(D_HALVES):
                     d_cols = slice(dh * N_MOVE, (dh + 1) * N_MOVE)
@@ -225,11 +225,13 @@ def tile_multidimensinalgrucell_pb_v_kernel(
                             start=(g == 0),
                             stop=(g == GATES - 1),
                         )
+            result = work.tile([P, P, D_TILES], F32, tag="result")
             for dh in range(D_HALVES):
-                d_cols = slice(dh * N_MOVE, (dh + 1) * N_MOVE)
-                result = work.tile([P, N_MOVE], F32, tag="result", bufs=4)
-                nc.scalar.copy(out=result[:], in_=accs[dh][:])
-                nc.sync.dma_start(out=out_rows[:, bt, d_cols], in_=result[:])
+                nc.scalar.copy(
+                    out=result[:, :, dh * TILES_PER_HALF : (dh + 1) * TILES_PER_HALF],
+                    in_=accs[dh][:].rearrange("b (j p) -> b p j", p=P),
+                )
+            nc.sync.dma_start(out=out_rows[:, bt, :], in_=result[:].rearrange("b p t -> b (p t)"))
 
         def start(bt):
             subtract_h(bt, 0, 2)
@@ -238,16 +240,17 @@ def tile_multidimensinalgrucell_pb_v_kernel(
 
         def first_gates(bt):
             times_z(bt, 0, 2)
-            turn_z(bt, 2)
-            turn_z(bt, 3)
+            if bt + 1 < B_TILES:
+                turn_z(bt + 1, 0)
+                turn_z(bt + 1, 1)
             times_grad(bt, 0, 2)
             subtract_h(bt, 2, 4)
 
         def last_gates(bt):
             times_z(bt, 2, 4)
             if bt + 1 < B_TILES:
-                turn_z(bt + 1, 0)
-                turn_z(bt + 1, 1)
+                turn_z(bt + 1, 2)
+                turn_z(bt + 1, 3)
             times_grad(bt, 2, 4)
             if bt + 1 < B_TILES:
                 turn_grad(bt + 1)
@@ -255,8 +258,8 @@ def tile_multidimensinalgrucell_pb_v_kernel(
         blend(nc.vector, 0)
         turn_v(0)
         turn_grad(0)
-        turn_z(0, 0)
-        turn_z(0, 1)
+        for g in range(GATES):
+            turn_z(0, g)
         turn_h(0)
         blend(nc.vector, 1)
         turn_v(1)

@@ -83,7 +83,8 @@ def tile_multidimensinalgrucell_pb_v_kernel(
 
         def load_weight(g):
             nc.sync.dma_start(
-                out=w_tiles[g][:], in_=weights[g][KD - D : KD, :].rearrange("(p t) u -> p t u", t=D_TILES)
+                out=w_tiles[g][:].rearrange("p (h j) u -> p h j u", h=D_HALVES),
+                in_=weights[g][KD - D : KD, :].rearrange("(h p j) u -> p h j u", h=D_HALVES, p=P),
             )
 
         load_two_batch_tiles(0)
@@ -157,9 +158,9 @@ def tile_multidimensinalgrucell_pb_v_kernel(
 
         def turn_grad(bt):
             words = grad_tiles[bt // 2][:].bitcast(F32)[:, bt % 2, :].rearrange("p (q c) -> p c q", c=2)
-            bank = psum.tile([P, 2, P], F32, tag="grad_bank", bufs=1)
+            bank = psum.tile([P, P, 2], F32, tag="grad_bank", bufs=1)
             for c in range(2):
-                nc.tensor.transpose(bank[:, c, :], words[:, c, :], identity[:])
+                nc.tensor.transpose(bank[:, :, c], words[:, c, :], identity[:])
             grad_banks[bt] = bank
 
         def turn_planes(bank, rows):
@@ -175,33 +176,33 @@ def tile_multidimensinalgrucell_pb_v_kernel(
             z_banks[(bt, g)] = psum.tile([P, PACK, P], F32, tag="z_bank", bufs=GATES, name="z_bank")
             turn_planes(z_banks[(bt, g)], z_tiles[bt][:, g, :])
 
-        def subtract_h(bt, lo, hi):
-            for g in range(lo, hi):
+        def subtract_h(bt):
+            for lo, hi in gate_pairs:
                 nc.vector.tensor_tensor(
-                    out=diff[bt % 2][:, g, :, :],
-                    in0=v_turned[bt][:, g, :, :],
-                    in1=h_banks[bt][:].rearrange("q t b -> q b t"),
+                    out=diff[bt % 2][:, lo:hi, :, :],
+                    in0=v_turned[bt][:, lo:hi, :, :],
+                    in1=h_banks[bt][:].rearrange("q t b -> q b t").unsqueeze(1).to_broadcast([P, 2, P, PACK]),
                     op=SUB,
                 )
 
-        def times_z(bt, lo, hi):
-            for g in range(lo, hi):
+        def times_z(bt):
+            for g in range(GATES):
                 nc.vector.tensor_tensor(
                     out=diff[bt % 2][:, g, :, :],
                     in0=diff[bt % 2][:, g, :, :],
                     in1=z_banks[(bt, g)][:].rearrange("q t b -> q b t"),
                     op=MULT,
                 )
+                if bt + 1 < B_TILES:
+                    turn_z(bt + 1, g)
 
         def times_grad(bt, lo, hi):
-            grad = grad_banks[bt][:].bitcast(BF16).rearrange("q c (b e) -> q b c e", e=2)
-            for g in range(lo, hi):
-                nc.vector.tensor_tensor(
-                    out=dg_grouped[bt % 2][:, g, :, :].rearrange("q b (c e) -> q b c e", e=2),
-                    in0=diff[bt % 2][:, g, :, :].rearrange("q b (c e) -> q b c e", e=2),
-                    in1=grad,
-                    op=MULT,
-                )
+            nc.vector.tensor_tensor(
+                out=dg_grouped[bt % 2][:, lo:hi, :, :],
+                in0=diff[bt % 2][:, lo:hi, :, :],
+                in1=grad_banks[bt][:].bitcast(BF16).unsqueeze(1).to_broadcast([P, hi - lo, P, PACK]),
+                op=MULT,
+            )
 
         def quantise_dg(bt, lo, hi):
             nc.vector.quantize_mx(
@@ -225,35 +226,12 @@ def tile_multidimensinalgrucell_pb_v_kernel(
                             start=(g == 0),
                             stop=(g == GATES - 1),
                         )
-            result = work.tile([P, P, D_TILES], F32, tag="result")
             for dh in range(D_HALVES):
-                nc.scalar.copy(
-                    out=result[:, :, dh * TILES_PER_HALF : (dh + 1) * TILES_PER_HALF],
-                    in_=accs[dh][:].rearrange("b (j p) -> b p j", p=P),
+                result = work.tile([P, P, TILES_PER_HALF], F32, tag="result", bufs=4)
+                nc.scalar.copy(out=result[:], in_=accs[dh][:].rearrange("b (j p) -> b p j", p=P))
+                nc.sync.dma_start(
+                    out=out_rows[:, bt, dh * N_MOVE : (dh + 1) * N_MOVE], in_=result[:].rearrange("b p j -> b (p j)")
                 )
-            nc.sync.dma_start(out=out_rows[:, bt, :], in_=result[:].rearrange("b p t -> b (p t)"))
-
-        def start(bt):
-            subtract_h(bt, 0, 2)
-            if bt > 0:
-                quantise_dg(bt - 1, 0, GATES)
-
-        def first_gates(bt):
-            times_z(bt, 0, 2)
-            if bt + 1 < B_TILES:
-                turn_z(bt + 1, 0)
-                turn_z(bt + 1, 1)
-            times_grad(bt, 0, 2)
-            subtract_h(bt, 2, 4)
-
-        def last_gates(bt):
-            times_z(bt, 2, 4)
-            if bt + 1 < B_TILES:
-                turn_z(bt + 1, 2)
-                turn_z(bt + 1, 3)
-            times_grad(bt, 2, 4)
-            if bt + 1 < B_TILES:
-                turn_grad(bt + 1)
 
         blend(nc.vector, 0)
         turn_v(0)
@@ -266,31 +244,43 @@ def tile_multidimensinalgrucell_pb_v_kernel(
         blend(nc.gpsimd, 2)
         blend(nc.gpsimd, 3)
         turn_weight(0)
-        start(0)
-        first_gates(0)
         turn_weight(1)
+        subtract_h(0)
         turn_h(1)
-        last_gates(0)
+        times_z(0)
+        times_grad(0, 0, 2)
+        times_grad(0, 2, 4)
+        turn_grad(1)
         turn_v(2)
-        start(1)
-        first_gates(1)
         turn_weight(2)
+
+        subtract_h(1)
+        quantise_dg(0, 0, GATES)
         turn_h(2)
-        last_gates(1)
         turn_weight(3)
+        times_z(1)
+        times_grad(1, 0, 2)
+        times_grad(1, 2, 4)
+        turn_grad(2)
         turn_v(3)
-        start(2)
+
+        subtract_h(2)
+        quantise_dg(1, 0, GATES)
         for g in range(GATES):
             quantise_weight(g)
-        first_gates(2)
         multiply_and_store(0)
         turn_h(3)
-        last_gates(2)
+        times_z(2)
+        times_grad(2, 0, 2)
+        times_grad(2, 2, 4)
+        turn_grad(3)
         multiply_and_store(1)
-        start(3)
-        first_gates(3)
-        quantise_dg(3, 0, 2)
+
+        subtract_h(3)
+        quantise_dg(2, 0, GATES)
         multiply_and_store(2)
-        last_gates(3)
-        quantise_dg(3, 2, 4)
+        times_z(3)
+        for lo, hi in gate_pairs:
+            times_grad(3, lo, hi)
+            quantise_dg(3, lo, hi)
         multiply_and_store(3)

@@ -89,12 +89,12 @@ def tile_multidimensinalgrucell_pb_v_kernel(
 
         load_two_batch_tiles(0)
         load_z(1)
+        load_two_batch_tiles(1)
         load_weight(0)
         load_weight(1)
-        load_two_batch_tiles(1)
+        load_z(3)
         load_weight(2)
         load_weight(3)
-        load_z(3)
 
         identity = keep.tile([P, P], F32, name="identity")
         make_identity(nc, identity[:])
@@ -136,14 +136,26 @@ def tile_multidimensinalgrucell_pb_v_kernel(
                 in_=w_grouped[g][:].rearrange("q d t -> q (d t)"),
             )
 
-        def blend(engine, bt):
-            z_t, v_t = z_tiles[bt], v_tiles[bt // 2][:, :, bt % 2, :]
-            prod = work.tile([P, GATES, U], F32, tag="prod")
-            part = work.tile([P, 2, U], F32, tag="part")
-            for g in range(GATES):
-                engine.tensor_tensor(out=prod[:, g, :], in0=z_t[:, g, :], in1=v_t[:, g, :], op=MULT)
-            for i in range(2):
-                engine.tensor_tensor(out=part[:, i, :], in0=prod[:, 2 * i, :], in1=prod[:, 2 * i + 1, :], op=ADD)
+        prod_tiles, part_tiles = {}, {}
+
+        def gate_products(engine, bt, lo, hi):
+            if lo == 0:
+                prod_tiles[bt] = work.tile([P, GATES, U], F32, tag="prod", name="prod")
+                part_tiles[bt] = work.tile([P, 2, U], F32, tag="part", name="part")
+            for g in range(lo, hi):
+                engine.tensor_tensor(
+                    out=prod_tiles[bt][:, g, :],
+                    in0=z_tiles[bt][:, g, :],
+                    in1=v_tiles[bt // 2][:, g, bt % 2, :],
+                    op=MULT,
+                )
+
+        def pair_sum(engine, bt, i):
+            prod = prod_tiles[bt]
+            engine.tensor_tensor(out=part_tiles[bt][:, i, :], in0=prod[:, 2 * i, :], in1=prod[:, 2 * i + 1, :], op=ADD)
+
+        def add_pairs(engine, bt):
+            part = part_tiles[bt]
             engine.tensor_tensor(out=h_tiles[bt][:], in0=part[:, 0, :], in1=part[:, 1, :], op=ADD)
 
         def turn_v(bt):
@@ -233,36 +245,45 @@ def tile_multidimensinalgrucell_pb_v_kernel(
                     out=out_rows[:, bt, dh * N_MOVE : (dh + 1) * N_MOVE], in_=result[:].rearrange("b p j -> b (p j)")
                 )
 
-        blend(nc.vector, 0)
+        gate_products(nc.vector, 0, 0, GATES)
+        pair_sum(nc.vector, 0, 0)
+        pair_sum(nc.vector, 0, 1)
+        gate_products(nc.vector, 1, 0, 2)
+        add_pairs(nc.vector, 0)
+        pair_sum(nc.vector, 1, 0)
+        gate_products(nc.gpsimd, 1, 2, GATES)
+        pair_sum(nc.gpsimd, 1, 1)
+        add_pairs(nc.gpsimd, 1)
+        for bt in range(2, B_TILES):
+            gate_products(nc.gpsimd, bt, 0, GATES)
+            pair_sum(nc.gpsimd, bt, 0)
+            pair_sum(nc.gpsimd, bt, 1)
+            add_pairs(nc.gpsimd, bt)
         turn_v(0)
         turn_grad(0)
         for g in range(GATES):
             turn_z(0, g)
         turn_h(0)
-        blend(nc.vector, 1)
-        turn_v(1)
-        blend(nc.gpsimd, 2)
-        blend(nc.gpsimd, 3)
-        turn_weight(0)
-        turn_weight(1)
+        for bt in range(1, B_TILES):
+            turn_v(bt)
         subtract_h(0)
         turn_h(1)
         times_z(0)
+        turn_weight(0)
         times_grad(0, 0, 2)
         times_grad(0, 2, 4)
         turn_grad(1)
-        turn_v(2)
-        turn_weight(2)
+        turn_weight(1)
 
         subtract_h(1)
         quantise_dg(0, 0, GATES)
         turn_h(2)
-        turn_weight(3)
         times_z(1)
         times_grad(1, 0, 2)
         times_grad(1, 2, 4)
         turn_grad(2)
-        turn_v(3)
+        turn_weight(2)
+        turn_weight(3)
 
         subtract_h(2)
         quantise_dg(1, 0, GATES)

@@ -81,14 +81,21 @@ def tile_multidimensinalgrucell_pb_v_kernel(
             for lo, hi in gate_pairs:
                 nc.sync.dma_start(out=z_tiles[bt][:, lo:hi, :], in_=z_rows[:, bt, lo:hi, :])
 
+        def load_one_batch_tile(bt):
+            for lo, hi in gate_pairs:
+                for g in range(lo, hi):
+                    nc.sync.dma_start(out=v_tiles[bt // 2][:, g, bt % 2, :], in_=blended_rows[g][:, bt, :])
+                nc.sync.dma_start(out=z_tiles[bt][:, lo:hi, :], in_=z_rows[:, bt, lo:hi, :])
+
         def load_weight(g):
             nc.sync.dma_start(
                 out=w_tiles[g][:].rearrange("p (h j) u -> p h j u", h=D_HALVES),
                 in_=weights[g][KD - D : KD, :].rearrange("(h p j) u -> p h j u", h=D_HALVES, p=P),
             )
 
-        load_two_batch_tiles(0)
-        load_z(1)
+        load_one_batch_tile(0)
+        nc.sync.dma_start(out=grad_tiles[0][:], in_=grad_rows[:, 0:2, :])
+        load_one_batch_tile(1)
         load_two_batch_tiles(1)
         load_weight(0)
         load_weight(1)
@@ -151,10 +158,14 @@ def tile_multidimensinalgrucell_pb_v_kernel(
                 )
 
         def pair_sum(engine, bt, i):
+            if bt in summed_by_tensor:
+                return
             prod = prod_tiles[bt]
             engine.tensor_tensor(out=part_tiles[bt][:, i, :], in0=prod[:, 2 * i, :], in1=prod[:, 2 * i + 1, :], op=ADD)
 
         def add_pairs(engine, bt):
+            if bt in summed_by_tensor:
+                return
             part = part_tiles[bt]
             engine.tensor_tensor(out=h_tiles[bt][:], in0=part[:, 0, :], in1=part[:, 1, :], op=ADD)
 
@@ -180,9 +191,24 @@ def tile_multidimensinalgrucell_pb_v_kernel(
             for t in range(PACK):
                 nc.tensor.transpose(bank[:, t, :], planes[:, t, :], identity[:])
 
+        summed_by_tensor = (0, 3)
+
         def turn_h(bt):
             h_banks[bt] = psum.tile([P, PACK, P], F32, tag="h_bank", bufs=1, name="h_bank")
-            turn_planes(h_banks[bt], h_tiles[bt][:])
+            if bt not in summed_by_tensor:
+                turn_planes(h_banks[bt], h_tiles[bt][:])
+                return
+            for g in range(GATES):
+                planes = prod_tiles[bt][:, g, :].rearrange("p (q t) -> p t q", t=PACK)
+                for t in range(PACK):
+                    nc.tensor.matmul(
+                        out=h_banks[bt][:, t, :],
+                        lhsT=planes[:, t, :],
+                        rhs=identity[:],
+                        is_transpose=True,
+                        start=(g == 0 and t == 0),
+                        stop=(g == GATES - 1 and t == PACK - 1),
+                    )
 
         def turn_z(bt, g):
             z_banks[(bt, g)] = psum.tile([P, PACK, P], F32, tag="z_bank", bufs=GATES, name="z_bank")
@@ -224,7 +250,12 @@ def tile_multidimensinalgrucell_pb_v_kernel(
             )
 
         def multiply_and_store(bt):
-            accs = [psum.tile([P, N_MOVE], F32, tag="stage", name="acc%d" % dh) for dh in range(D_HALVES)]
+            if bt < 2:
+                accs = [psum.tile([P, N_MOVE], F32, tag="stage", name="acc%d" % dh) for dh in range(D_HALVES)]
+            else:
+                accs = [
+                    psum.tile([P, N_MOVE], F32, tag="z_bank", bufs=GATES, name="late_acc%d" % dh) for dh in range(D_HALVES)
+                ]
             for lo, hi in gate_pairs:
                 for dh in range(D_HALVES):
                     d_cols = slice(dh * N_MOVE, (dh + 1) * N_MOVE)
@@ -287,20 +318,20 @@ def tile_multidimensinalgrucell_pb_v_kernel(
 
         subtract_h(2)
         quantise_dg(1, 0, GATES)
-        for g in range(GATES):
-            quantise_weight(g)
-        multiply_and_store(0)
         turn_h(3)
         times_z(2)
         times_grad(2, 0, 2)
         times_grad(2, 2, 4)
         turn_grad(3)
-        multiply_and_store(1)
+        for g in range(GATES):
+            quantise_weight(g)
+        multiply_and_store(0)
 
         subtract_h(3)
         quantise_dg(2, 0, GATES)
-        multiply_and_store(2)
+        multiply_and_store(1)
         times_z(3)
+        multiply_and_store(2)
         for lo, hi in gate_pairs:
             times_grad(3, lo, hi)
             quantise_dg(3, lo, hi)

@@ -94,8 +94,8 @@ def tile_multidimensinalgrucell_pb_v_kernel(
             )
 
         load_one_batch_tile(0)
-        nc.sync.dma_start(out=grad_tiles[0][:], in_=grad_rows[:, 0:2, :])
         load_one_batch_tile(1)
+        nc.sync.dma_start(out=grad_tiles[0][:], in_=grad_rows[:, 0:2, :])
         load_two_batch_tiles(1)
         load_weight(0)
         load_weight(1)
@@ -249,14 +249,14 @@ def tile_multidimensinalgrucell_pb_v_kernel(
                 in_=dg_grouped[bt % 2][:, lo:hi, :, :].rearrange("q g b t -> q (g b t)"),
             )
 
-        def multiply_and_store(bt):
+        def multiply_and_store(bt, groups):
             if bt < 2:
                 accs = [psum.tile([P, N_MOVE], F32, tag="stage", name="acc%d" % dh) for dh in range(D_HALVES)]
             else:
                 accs = [
                     psum.tile([P, N_MOVE], F32, tag="z_bank", bufs=GATES, name="late_acc%d" % dh) for dh in range(D_HALVES)
                 ]
-            for lo, hi in gate_pairs:
+            for lo, hi in groups:
                 for dh in range(D_HALVES):
                     d_cols = slice(dh * N_MOVE, (dh + 1) * N_MOVE)
                     for g in range(lo, hi):
@@ -277,10 +277,13 @@ def tile_multidimensinalgrucell_pb_v_kernel(
                 )
 
         gate_products(nc.vector, 0, 0, GATES)
-        pair_sum(nc.vector, 0, 0)
-        pair_sum(nc.vector, 0, 1)
+        turn_v(0)
+        turn_h(0)
+        for g in range(GATES):
+            turn_z(0, g)
+        turn_grad(0)
+        subtract_h(0)
         gate_products(nc.vector, 1, 0, 2)
-        add_pairs(nc.vector, 0)
         pair_sum(nc.vector, 1, 0)
         gate_products(nc.gpsimd, 1, 2, GATES)
         pair_sum(nc.gpsimd, 1, 1)
@@ -290,14 +293,8 @@ def tile_multidimensinalgrucell_pb_v_kernel(
             pair_sum(nc.gpsimd, bt, 0)
             pair_sum(nc.gpsimd, bt, 1)
             add_pairs(nc.gpsimd, bt)
-        turn_v(0)
-        turn_grad(0)
-        for g in range(GATES):
-            turn_z(0, g)
-        turn_h(0)
         for bt in range(1, B_TILES):
             turn_v(bt)
-        subtract_h(0)
         turn_h(1)
         times_z(0)
         turn_weight(0)
@@ -325,14 +322,14 @@ def tile_multidimensinalgrucell_pb_v_kernel(
         turn_grad(3)
         for g in range(GATES):
             quantise_weight(g)
-        multiply_and_store(0)
+        multiply_and_store(0, [(0, GATES)])
 
         subtract_h(3)
         quantise_dg(2, 0, GATES)
-        multiply_and_store(1)
+        multiply_and_store(1, [(0, GATES)])
         times_z(3)
-        multiply_and_store(2)
+        multiply_and_store(2, [(0, GATES)])
         for lo, hi in gate_pairs:
             times_grad(3, lo, hi)
             quantise_dg(3, lo, hi)
-        multiply_and_store(3)
+        multiply_and_store(3, gate_pairs)

@@ -71,21 +71,19 @@ def tile_multidimensinalgrucell_pb_v_kernel(
         w_tiles = [inputs.tile([P, D_TILES, U], BF16, name="w%d" % g) for g in range(GATES)]
 
         def load_two_batch_tiles(i):
-            for lo, hi in gate_pairs:
-                for g in range(lo, hi):
-                    nc.sync.dma_start(out=v_tiles[i][:, g, :, :], in_=blended_rows[g][:, 2 * i : 2 * i + 2, :])
-                nc.sync.dma_start(out=z_tiles[2 * i][:, lo:hi, :], in_=z_rows[:, 2 * i, lo:hi, :])
+            for g in range(GATES):
+                nc.sync.dma_start(out=v_tiles[i][:, g, :, :], in_=blended_rows[g][:, 2 * i : 2 * i + 2, :])
+                nc.sync.dma_start(out=z_tiles[2 * i][:, g, :], in_=z_rows[:, 2 * i, g, :])
             nc.sync.dma_start(out=grad_tiles[i][:], in_=grad_rows[:, 2 * i : 2 * i + 2, :])
 
         def load_z(bt):
-            for lo, hi in gate_pairs:
-                nc.sync.dma_start(out=z_tiles[bt][:, lo:hi, :], in_=z_rows[:, bt, lo:hi, :])
+            for g in range(GATES):
+                nc.sync.dma_start(out=z_tiles[bt][:, g, :], in_=z_rows[:, bt, g, :])
 
         def load_one_batch_tile(bt):
-            for lo, hi in gate_pairs:
-                for g in range(lo, hi):
-                    nc.sync.dma_start(out=v_tiles[bt // 2][:, g, bt % 2, :], in_=blended_rows[g][:, bt, :])
-                nc.sync.dma_start(out=z_tiles[bt][:, lo:hi, :], in_=z_rows[:, bt, lo:hi, :])
+            for g in range(GATES):
+                nc.sync.dma_start(out=v_tiles[bt // 2][:, g, bt % 2, :], in_=blended_rows[g][:, bt, :])
+                nc.sync.dma_start(out=z_tiles[bt][:, g, :], in_=z_rows[:, bt, g, :])
 
         def load_weight(g):
             nc.sync.dma_start(
@@ -98,10 +96,9 @@ def tile_multidimensinalgrucell_pb_v_kernel(
         nc.sync.dma_start(out=grad_tiles[0][:], in_=grad_rows[:, 0:2, :])
         load_two_batch_tiles(1)
         load_weight(0)
-        load_weight(1)
         load_z(3)
-        load_weight(2)
-        load_weight(3)
+        for g in range(1, GATES):
+            load_weight(g)
 
         identity = keep.tile([P, P], F32, name="identity")
         make_identity(nc, identity[:])
@@ -114,18 +111,23 @@ def tile_multidimensinalgrucell_pb_v_kernel(
             keep.tile([P, D, PACK], BF16, name="w_grouped%d" % g, align_bytes=64) for g in range(GATES)
         ]
         dg_grouped = [
-            keep.tile([P, GATES, P, PACK], BF16, name="dg_grouped%d" % i, align_bytes=64) for i in range(2)
+            keep.tile([P, GATES, P, PACK], BF16, name="dg_grouped%d" % i, align_bytes=64) for i in range(B_TILES)
         ]
-        h_tiles = [keep.tile([P, U], F32, name="h%d" % bt) for bt in range(B_TILES)]
-        v_turned = [keep.tile([P, GATES, P, PACK], BF16, name="v_turned%d" % bt) for bt in range(B_TILES)]
+        h_rows = keep.tile([P, U], F32, name="h_rows")
+        h_part = keep.tile([P, 2, U], F32, name="h_part")
+        dg_rows = keep.tile([P, GATES, U], BF16, name="dg_rows")
+        grad_turned = keep.tile([P, P, PACK], BF16, name="grad_turned")
+        v_turned = [keep.tile([P, GATES, P, PACK], BF16, name="v_turned%d" % bt) for bt in range(B_TILES - 1)]
         diff = [keep.tile([P, GATES, P, PACK], F32, name="diff%d" % i) for i in range(2)]
+        H_BANK, G_BANK, Z_BANK, S_BANK = ("h_bank", 1), ("grad_bank", 1), ("z_bank", GATES), ("stage", 2)
+        acc_banks = [(S_BANK, S_BANK), (H_BANK, G_BANK), (Z_BANK, Z_BANK), (Z_BANK, Z_BANK)]
         h_banks, grad_banks, z_banks = {}, {}, {}
 
-        def turn_weight(g):
+        def turn_weight(g, bank):
             words = w_tiles[g][:].bitcast(F32).rearrange("p t (q c) -> p t c q", c=2)
             grouped_words = w_grouped[g][:].bitcast(F32)
             for two in range(D_TILES // 2):
-                turned = psum.tile([P, 2, 2 * P], F32, tag="stage")
+                turned = psum.tile([P, 2, 2 * P], F32, tag=bank[0], bufs=bank[1], name="turned")
                 for j in range(2):
                     for c in range(2):
                         nc.tensor.transpose(
@@ -143,12 +145,11 @@ def tile_multidimensinalgrucell_pb_v_kernel(
                 in_=w_grouped[g][:].rearrange("q d t -> q (d t)"),
             )
 
-        prod_tiles, part_tiles = {}, {}
+        prod_tiles = {}
 
         def gate_products(engine, bt, lo, hi):
             if lo == 0:
-                prod_tiles[bt] = work.tile([P, GATES, U], F32, tag="prod", name="prod")
-                part_tiles[bt] = work.tile([P, 2, U], F32, tag="part", name="part")
+                prod_tiles[bt] = work.tile([P, GATES, U], F32, tag="prod", name="prod", bufs=3)
             for g in range(lo, hi):
                 engine.tensor_tensor(
                     out=prod_tiles[bt][:, g, :],
@@ -157,17 +158,42 @@ def tile_multidimensinalgrucell_pb_v_kernel(
                     op=MULT,
                 )
 
-        def pair_sum(engine, bt, i):
-            if bt in summed_by_tensor:
-                return
+        def sum_products(engine, bt):
             prod = prod_tiles[bt]
-            engine.tensor_tensor(out=part_tiles[bt][:, i, :], in0=prod[:, 2 * i, :], in1=prod[:, 2 * i + 1, :], op=ADD)
+            engine.tensor_tensor(out=h_part[:], in0=prod[:, 0:2, :], in1=prod[:, 2:4, :], op=ADD)
+            engine.tensor_tensor(out=h_rows[:], in0=h_part[:, 0, :], in1=h_part[:, 1, :], op=ADD)
 
-        def add_pairs(engine, bt):
-            if bt in summed_by_tensor:
-                return
-            part = part_tiles[bt]
-            engine.tensor_tensor(out=h_tiles[bt][:], in0=part[:, 0, :], in1=part[:, 1, :], op=ADD)
+        def subtract_h_rows(bt):
+            nc.vector.tensor_tensor(
+                out=diff[bt % 2][:].rearrange("p g b t -> p g (b t)"),
+                in0=v_tiles[bt // 2][:, :, bt % 2, :],
+                in1=h_rows[:].unsqueeze(1).to_broadcast([P, GATES, U]),
+                op=SUB,
+            )
+
+        def times_z_rows(bt, lo, hi):
+            rows = diff[bt % 2][:].rearrange("p g b t -> p g (b t)")[:, lo:hi, :]
+            nc.vector.tensor_tensor(out=rows, in0=rows, in1=z_tiles[bt][:, lo:hi, :], op=MULT)
+
+        def times_grad_rows(bt, lo, hi):
+            rows = diff[bt % 2][:].rearrange("p g b t -> p g (b t)")
+            nc.vector.tensor_tensor(
+                out=dg_rows[:, lo:hi, :],
+                in0=rows[:, lo:hi, :],
+                in1=grad_tiles[bt // 2][:, bt % 2, :].unsqueeze(1).to_broadcast([P, hi - lo, U]),
+                op=MULT,
+            )
+
+        def turn_dg(bt, lo, hi):
+            words = dg_rows[:].bitcast(F32).rearrange("p g (q c) -> p g c q", c=2)
+            turned = psum.tile([P, 2, 2, P], F32, tag="stage")
+            for g in range(lo, hi):
+                for c in range(2):
+                    nc.tensor.transpose(turned[:, g - lo, c, :], words[:, g, c, :], identity[:])
+            nc.scalar.copy(
+                out=dg_grouped[bt][:].bitcast(F32)[:, lo:hi, :, :],
+                in_=turned[:, 0 : hi - lo, :, :].rearrange("q g c b -> q g b c"),
+            )
 
         def turn_v(bt):
             words = v_tiles[bt // 2][:].bitcast(F32)[:, :, bt % 2, :].rearrange("p g (q c) -> p g c q", c=2)
@@ -185,19 +211,16 @@ def tile_multidimensinalgrucell_pb_v_kernel(
             for c in range(2):
                 nc.tensor.transpose(bank[:, :, c], words[:, c, :], identity[:])
             grad_banks[bt] = bank
+            if bt == 2:
+                nc.scalar.copy(out=grad_turned[:].bitcast(F32), in_=bank[:])
 
         def turn_planes(bank, rows):
             planes = rows.rearrange("p (q t) -> p t q", t=PACK)
             for t in range(PACK):
                 nc.tensor.transpose(bank[:, t, :], planes[:, t, :], identity[:])
 
-        summed_by_tensor = (0, 3)
-
         def turn_h(bt):
             h_banks[bt] = psum.tile([P, PACK, P], F32, tag="h_bank", bufs=1, name="h_bank")
-            if bt not in summed_by_tensor:
-                turn_planes(h_banks[bt], h_tiles[bt][:])
-                return
             for g in range(GATES):
                 planes = prod_tiles[bt][:, g, :].rearrange("p (q t) -> p t q", t=PACK)
                 for t in range(PACK):
@@ -231,50 +254,63 @@ def tile_multidimensinalgrucell_pb_v_kernel(
                     in1=z_banks[(bt, g)][:].rearrange("q t b -> q b t"),
                     op=MULT,
                 )
-                if bt + 1 < B_TILES:
+                if bt + 1 < 3:
                     turn_z(bt + 1, g)
 
         def times_grad(bt, lo, hi):
             nc.vector.tensor_tensor(
-                out=dg_grouped[bt % 2][:, lo:hi, :, :],
+                out=dg_grouped[bt][:, lo:hi, :, :],
                 in0=diff[bt % 2][:, lo:hi, :, :],
                 in1=grad_banks[bt][:].bitcast(BF16).unsqueeze(1).to_broadcast([P, hi - lo, P, PACK]),
                 op=MULT,
             )
 
+        def times_grad_gpsimd(bt, lo, hi):
+            for g in range(lo, hi):
+                nc.gpsimd.tensor_tensor(
+                    out=dg_grouped[bt][:, g, :, :], in0=diff[bt % 2][:, g, :, :], in1=grad_turned[:], op=MULT
+                )
+
         def quantise_dg(bt, lo, hi):
             nc.vector.quantize_mx(
                 out=dg_codes[:, bt, lo:hi, :].rearrange("q g b -> q (g b)").bitcast(E5M2_X4),
                 scales=dg_scales[:, bt, lo:hi, :].rearrange("q g b -> q (g b)"),
-                in_=dg_grouped[bt % 2][:, lo:hi, :, :].rearrange("q g b t -> q (g b t)"),
+                in_=dg_grouped[bt][:, lo:hi, :, :].rearrange("q g b t -> q (g b t)"),
             )
 
-        def multiply_and_store(bt, groups):
-            if bt < 2:
-                accs = [psum.tile([P, N_MOVE], F32, tag="stage", name="acc%d" % dh) for dh in range(D_HALVES)]
-            else:
-                accs = [
-                    psum.tile([P, N_MOVE], F32, tag="z_bank", bufs=GATES, name="late_acc%d" % dh) for dh in range(D_HALVES)
-                ]
-            for lo, hi in groups:
-                for dh in range(D_HALVES):
-                    d_cols = slice(dh * N_MOVE, (dh + 1) * N_MOVE)
-                    for g in range(lo, hi):
-                        nc.tensor.matmul_mx(
-                            out=accs[dh][:],
-                            lhsT=dg_codes[:, bt, g, :].bitcast(E5M2_X4),
-                            lhsT_scale=dg_scales[:, bt, g, :],
-                            rhs=w_codes[:, g, d_cols].bitcast(E4M3_X4),
-                            rhs_scale=w_scales[:, g, d_cols],
-                            start=(g == 0),
-                            stop=(g == GATES - 1),
-                        )
+        acc_tiles = {}
+
+        def open_sums(bt):
+            acc_tiles[bt] = []
+            for tag, bufs in acc_banks[bt]:
+                acc_tiles[bt].append(psum.tile([P, N_MOVE], F32, tag=tag, bufs=bufs, name="acc"))
+
+        def multiply(bt, lo, hi, first, last):
+            for dh in range(D_HALVES):
+                d_cols = slice(dh * N_MOVE, (dh + 1) * N_MOVE)
+                for g in range(lo, hi):
+                    nc.tensor.matmul_mx(
+                        out=acc_tiles[bt][dh][:],
+                        lhsT=dg_codes[:, bt, g, :].bitcast(E5M2_X4),
+                        lhsT_scale=dg_scales[:, bt, g, :],
+                        rhs=w_codes[:, g, d_cols].bitcast(E4M3_X4),
+                        rhs_scale=w_scales[:, g, d_cols],
+                        start=(g == first),
+                        stop=(g == last),
+                    )
+
+        def store(bt):
             for dh in range(D_HALVES):
                 result = work.tile([P, P, TILES_PER_HALF], F32, tag="result", bufs=4)
-                nc.scalar.copy(out=result[:], in_=accs[dh][:].rearrange("b (j p) -> b p j", p=P))
+                nc.scalar.copy(out=result[:], in_=acc_tiles[bt][dh][:].rearrange("b (j p) -> b p j", p=P))
                 nc.sync.dma_start(
                     out=out_rows[:, bt, dh * N_MOVE : (dh + 1) * N_MOVE], in_=result[:].rearrange("b p j -> b (p j)")
                 )
+
+        def multiply_and_store(bt):
+            open_sums(bt)
+            multiply(bt, 0, GATES, 0, GATES - 1)
+            store(bt)
 
         gate_products(nc.vector, 0, 0, GATES)
         turn_v(0)
@@ -282,54 +318,54 @@ def tile_multidimensinalgrucell_pb_v_kernel(
         for g in range(GATES):
             turn_z(0, g)
         turn_grad(0)
+        gate_products(nc.vector, 1, 0, 1)
         subtract_h(0)
-        gate_products(nc.vector, 1, 0, 2)
-        pair_sum(nc.vector, 1, 0)
-        gate_products(nc.gpsimd, 1, 2, GATES)
-        pair_sum(nc.gpsimd, 1, 1)
-        add_pairs(nc.gpsimd, 1)
-        for bt in range(2, B_TILES):
+        gate_products(nc.gpsimd, 1, 1, GATES)
+        for bt in range(2, 4):
             gate_products(nc.gpsimd, bt, 0, GATES)
-            pair_sum(nc.gpsimd, bt, 0)
-            pair_sum(nc.gpsimd, bt, 1)
-            add_pairs(nc.gpsimd, bt)
-        for bt in range(1, B_TILES):
-            turn_v(bt)
+        sum_products(nc.gpsimd, 3)
+        turn_v(1)
         turn_h(1)
         times_z(0)
-        turn_weight(0)
         times_grad(0, 0, 2)
         times_grad(0, 2, 4)
         turn_grad(1)
-        turn_weight(1)
-
+        turn_v(2)
         subtract_h(1)
-        quantise_dg(0, 0, GATES)
+        turn_weight(0, S_BANK)
         turn_h(2)
         times_z(1)
         times_grad(1, 0, 2)
         times_grad(1, 2, 4)
         turn_grad(2)
-        turn_weight(2)
-        turn_weight(3)
-
+        turn_weight(1, S_BANK)
         subtract_h(2)
-        quantise_dg(1, 0, GATES)
-        turn_h(3)
         times_z(2)
-        times_grad(2, 0, 2)
+        times_grad_gpsimd(2, 0, 2)
         times_grad(2, 2, 4)
-        turn_grad(3)
+        turn_weight(2, Z_BANK)
+        turn_weight(3, Z_BANK)
+        quantise_dg(0, 0, GATES)
+        quantise_dg(1, 0, GATES)
         for g in range(GATES):
             quantise_weight(g)
-        multiply_and_store(0, [(0, GATES)])
-
-        subtract_h(3)
+        multiply_and_store(0)
+        multiply_and_store(1)
+        subtract_h_rows(3)
         quantise_dg(2, 0, GATES)
-        multiply_and_store(1, [(0, GATES)])
-        times_z(3)
-        multiply_and_store(2, [(0, GATES)])
-        for lo, hi in gate_pairs:
-            times_grad(3, lo, hi)
-            quantise_dg(3, lo, hi)
-        multiply_and_store(3, gate_pairs)
+        multiply_and_store(2)
+        times_z_rows(3, 0, 2)
+        times_z_rows(3, 2, 4)
+        open_sums(3)
+        for g in range(GATES):
+            times_grad_rows(3, g, g + 1)
+            if g == 3:
+                multiply(3, 0, 1, 0, 3)
+            turn_dg(3, g, g + 1)
+            if g >= 2:
+                quantise_dg(3, g - 2, g - 1)
+        quantise_dg(3, 2, 3)
+        quantise_dg(3, 3, 4)
+        for g in range(1, GATES):
+            multiply(3, g, g + 1, 0, 3)
+        store(3)

@@ -70,20 +70,17 @@ def tile_multidimensinalgrucell_pb_v_kernel(
         grad_tiles = [inputs.tile([P, 2, U], BF16, name="grad%d" % i) for i in range(B_TILES // 2)]
         w_tiles = [inputs.tile([P, D_TILES, U], BF16, name="w%d" % g) for g in range(GATES)]
 
-        def load_two_batch_tiles(i):
-            for g in range(GATES):
-                nc.sync.dma_start(out=v_tiles[i][:, g, :, :], in_=blended_rows[g][:, 2 * i : 2 * i + 2, :])
-                nc.sync.dma_start(out=z_tiles[2 * i][:, g, :], in_=z_rows[:, 2 * i, g, :])
+        def load_v(bt, g):
+            nc.sync.dma_start(out=v_tiles[bt // 2][:, g, bt % 2, :], in_=blended_rows[g][:, bt, :])
+
+        def load_v_pair(i, g):
+            nc.sync.dma_start(out=v_tiles[i][:, g, :, :], in_=blended_rows[g][:, 2 * i : 2 * i + 2, :])
+
+        def load_z(bt, lo, hi):
+            nc.sync.dma_start(out=z_tiles[bt][:, lo:hi, :], in_=z_rows[:, bt, lo:hi, :])
+
+        def load_grad(i):
             nc.sync.dma_start(out=grad_tiles[i][:], in_=grad_rows[:, 2 * i : 2 * i + 2, :])
-
-        def load_z(bt):
-            for g in range(GATES):
-                nc.sync.dma_start(out=z_tiles[bt][:, g, :], in_=z_rows[:, bt, g, :])
-
-        def load_one_batch_tile(bt):
-            for g in range(GATES):
-                nc.sync.dma_start(out=v_tiles[bt // 2][:, g, bt % 2, :], in_=blended_rows[g][:, bt, :])
-                nc.sync.dma_start(out=z_tiles[bt][:, g, :], in_=z_rows[:, bt, g, :])
 
         def load_weight(g):
             nc.sync.dma_start(
@@ -91,13 +88,22 @@ def tile_multidimensinalgrucell_pb_v_kernel(
                 in_=weights[g][KD - D : KD, :].rearrange("(h p j) u -> p h j u", h=D_HALVES, p=P),
             )
 
-        load_one_batch_tile(0)
-        load_one_batch_tile(1)
-        nc.sync.dma_start(out=grad_tiles[0][:], in_=grad_rows[:, 0:2, :])
-        load_two_batch_tiles(1)
-        load_weight(0)
-        load_z(3)
-        for g in range(1, GATES):
+        for g in range(GATES):
+            load_v(0, g)
+            load_z(0, g, g + 1)
+        for lo, hi in gate_pairs:
+            for g in range(lo, hi):
+                load_v(1, g)
+            load_z(1, lo, hi)
+        load_grad(0)
+        for lo, hi in gate_pairs:
+            for g in range(lo, hi):
+                load_v_pair(1, g)
+            load_z(2, lo, hi)
+        load_grad(1)
+        for lo, hi in gate_pairs:
+            load_z(3, lo, hi)
+        for g in range(GATES):
             load_weight(g)
 
         identity = keep.tile([P, P], F32, name="identity")
@@ -195,10 +201,10 @@ def tile_multidimensinalgrucell_pb_v_kernel(
                 in_=turned[:, 0 : hi - lo, :, :].rearrange("q g c b -> q g b c"),
             )
 
-        def turn_v(bt):
+        def turn_v(bt, pairs=gate_pairs):
             words = v_tiles[bt // 2][:].bitcast(F32)[:, :, bt % 2, :].rearrange("p g (q c) -> p g c q", c=2)
             turned_words = v_turned[bt][:].bitcast(F32)
-            for lo, hi in gate_pairs:
+            for lo, hi in pairs:
                 turned = psum.tile([P, 2, 2, P], F32, tag="stage")
                 for g in range(lo, hi):
                     for c in range(2):
@@ -219,9 +225,10 @@ def tile_multidimensinalgrucell_pb_v_kernel(
             for t in range(PACK):
                 nc.tensor.transpose(bank[:, t, :], planes[:, t, :], identity[:])
 
-        def turn_h(bt):
-            h_banks[bt] = psum.tile([P, PACK, P], F32, tag="h_bank", bufs=1, name="h_bank")
-            for g in range(GATES):
+        def turn_h(bt, lo=0, hi=GATES):
+            if lo == 0:
+                h_banks[bt] = psum.tile([P, PACK, P], F32, tag="h_bank", bufs=1, name="h_bank")
+            for g in range(lo, hi):
                 planes = prod_tiles[bt][:, g, :].rearrange("p (q t) -> p t q", t=PACK)
                 for t in range(PACK):
                     nc.tensor.matmul(
@@ -313,14 +320,14 @@ def tile_multidimensinalgrucell_pb_v_kernel(
             store(bt)
 
         gate_products(nc.vector, 0, 0, GATES)
-        turn_v(0)
-        turn_h(0)
+        for lo, hi in gate_pairs:
+            turn_v(0, [(lo, hi)])
+            turn_h(0, lo, hi)
         for g in range(GATES):
             turn_z(0, g)
         turn_grad(0)
-        gate_products(nc.vector, 1, 0, 1)
         subtract_h(0)
-        gate_products(nc.gpsimd, 1, 1, GATES)
+        gate_products(nc.gpsimd, 1, 0, GATES)
         for bt in range(2, 4):
             gate_products(nc.gpsimd, bt, 0, GATES)
         sum_products(nc.gpsimd, 3)
@@ -332,11 +339,11 @@ def tile_multidimensinalgrucell_pb_v_kernel(
         turn_grad(1)
         turn_v(2)
         subtract_h(1)
-        turn_weight(0, S_BANK)
         turn_h(2)
         times_z(1)
         times_grad(1, 0, 2)
         times_grad(1, 2, 4)
+        turn_weight(0, S_BANK)
         turn_grad(2)
         turn_weight(1, S_BANK)
         subtract_h(2)

@@ -120,13 +120,12 @@ def tile_multidimensinalgrucell_pb_v_kernel(
             keep.tile([P, GATES, P, PACK], BF16, name="dg_grouped%d" % i, align_bytes=64) for i in range(B_TILES)
         ]
         h_rows = keep.tile([P, U], F32, name="h_rows")
-        h_part = keep.tile([P, 2, U], F32, name="h_part")
-        dg_rows = keep.tile([P, GATES, U], BF16, name="dg_rows")
+        dg_rows = keep.tile([P, 2, U], BF16, name="dg_rows")
         grad_turned = keep.tile([P, P, PACK], BF16, name="grad_turned")
-        v_turned = [keep.tile([P, GATES, P, PACK], BF16, name="v_turned%d" % bt) for bt in range(B_TILES - 1)]
+        v_turned = [keep.tile([P, GATES, P, PACK], BF16, name="v_turned%d" % bt) for bt in range(B_TILES)]
         diff = [keep.tile([P, GATES, P, PACK], F32, name="diff%d" % i) for i in range(2)]
         H_BANK, G_BANK, Z_BANK, S_BANK = ("h_bank", 1), ("grad_bank", 1), ("z_bank", GATES), ("stage", 2)
-        acc_banks = [(S_BANK, S_BANK), (H_BANK, G_BANK), (Z_BANK, Z_BANK), (Z_BANK, Z_BANK)]
+        acc_banks = [(S_BANK, S_BANK), (Z_BANK, Z_BANK), (S_BANK, S_BANK), (Z_BANK, Z_BANK)]
         h_banks, grad_banks, z_banks = {}, {}, {}
 
         def turn_weight(g, bank):
@@ -166,14 +165,14 @@ def tile_multidimensinalgrucell_pb_v_kernel(
 
         def sum_products(engine, bt):
             prod = prod_tiles[bt]
-            engine.tensor_tensor(out=h_part[:], in0=prod[:, 0:2, :], in1=prod[:, 2:4, :], op=ADD)
-            engine.tensor_tensor(out=h_rows[:], in0=h_part[:, 0, :], in1=h_part[:, 1, :], op=ADD)
+            engine.tensor_tensor(out=prod[:, 0:2, :], in0=prod[:, 0:2, :], in1=prod[:, 2:4, :], op=ADD)
+            engine.tensor_tensor(out=h_rows[:], in0=prod[:, 0, :], in1=prod[:, 1, :], op=ADD)
 
-        def subtract_h_rows(bt):
+        def subtract_h_rows(bt, lo, hi):
             nc.vector.tensor_tensor(
-                out=diff[bt % 2][:].rearrange("p g b t -> p g (b t)"),
-                in0=v_tiles[bt // 2][:, :, bt % 2, :],
-                in1=h_rows[:].unsqueeze(1).to_broadcast([P, GATES, U]),
+                out=diff[bt % 2][:].rearrange("p g b t -> p g (b t)")[:, lo:hi, :],
+                in0=v_tiles[bt // 2][:, lo:hi, bt % 2, :],
+                in1=h_rows[:].unsqueeze(1).to_broadcast([P, hi - lo, U]),
                 op=SUB,
             )
 
@@ -183,16 +182,14 @@ def tile_multidimensinalgrucell_pb_v_kernel(
 
         def times_grad_rows(bt, lo, hi):
             rows = diff[bt % 2][:].rearrange("p g b t -> p g (b t)")
-            nc.vector.tensor_tensor(
-                out=dg_rows[:, lo:hi, :],
-                in0=rows[:, lo:hi, :],
-                in1=grad_tiles[bt // 2][:, bt % 2, :].unsqueeze(1).to_broadcast([P, hi - lo, U]),
-                op=MULT,
-            )
+            for g in range(lo, hi):
+                nc.gpsimd.tensor_tensor(
+                    out=dg_rows[:, g, :], in0=rows[:, g, :], in1=grad_tiles[bt // 2][:, bt % 2, :], op=MULT
+                )
 
         def turn_dg(bt, lo, hi):
             words = dg_rows[:].bitcast(F32).rearrange("p g (q c) -> p g c q", c=2)
-            turned = psum.tile([P, 2, 2, P], F32, tag="stage")
+            turned = psum.tile([P, 2, 2, P], F32, tag="h_bank", bufs=1, name="turned_dg")
             for g in range(lo, hi):
                 for c in range(2):
                     nc.tensor.transpose(turned[:, g - lo, c, :], words[:, g, c, :], identity[:])
@@ -228,6 +225,9 @@ def tile_multidimensinalgrucell_pb_v_kernel(
         def turn_h(bt, lo=0, hi=GATES):
             if lo == 0:
                 h_banks[bt] = psum.tile([P, PACK, P], F32, tag="h_bank", bufs=1, name="h_bank")
+            if bt == 3:
+                turn_planes(h_banks[bt], h_rows[:])
+                return
             for g in range(lo, hi):
                 planes = prod_tiles[bt][:, g, :].rearrange("p (q t) -> p t q", t=PACK)
                 for t in range(PACK):
@@ -244,8 +244,8 @@ def tile_multidimensinalgrucell_pb_v_kernel(
             z_banks[(bt, g)] = psum.tile([P, PACK, P], F32, tag="z_bank", bufs=GATES, name="z_bank")
             turn_planes(z_banks[(bt, g)], z_tiles[bt][:, g, :])
 
-        def subtract_h(bt):
-            for lo, hi in gate_pairs:
+        def subtract_h(bt, pairs=gate_pairs):
+            for lo, hi in pairs:
                 nc.vector.tensor_tensor(
                     out=diff[bt % 2][:, lo:hi, :, :],
                     in0=v_turned[bt][:, lo:hi, :, :],
@@ -253,8 +253,8 @@ def tile_multidimensinalgrucell_pb_v_kernel(
                     op=SUB,
                 )
 
-        def times_z(bt):
-            for g in range(GATES):
+        def times_z(bt, lo=0, hi=GATES):
+            for g in range(lo, hi):
                 nc.vector.tensor_tensor(
                     out=diff[bt % 2][:, g, :, :],
                     in0=diff[bt % 2][:, g, :, :],
@@ -292,8 +292,8 @@ def tile_multidimensinalgrucell_pb_v_kernel(
             for tag, bufs in acc_banks[bt]:
                 acc_tiles[bt].append(psum.tile([P, N_MOVE], F32, tag=tag, bufs=bufs, name="acc"))
 
-        def multiply(bt, lo, hi, first, last):
-            for dh in range(D_HALVES):
+        def multiply(bt, lo, hi, first, last, halves=range(D_HALVES)):
+            for dh in halves:
                 d_cols = slice(dh * N_MOVE, (dh + 1) * N_MOVE)
                 for g in range(lo, hi):
                     nc.tensor.matmul_mx(
@@ -306,9 +306,9 @@ def tile_multidimensinalgrucell_pb_v_kernel(
                         stop=(g == last),
                     )
 
-        def store(bt):
-            for dh in range(D_HALVES):
-                result = work.tile([P, P, TILES_PER_HALF], F32, tag="result", bufs=4)
+        def store(bt, halves=range(D_HALVES)):
+            for dh in halves:
+                result = work.tile([P, P, TILES_PER_HALF], F32, tag="result", bufs=6)
                 nc.scalar.copy(out=result[:], in_=acc_tiles[bt][dh][:].rearrange("b (j p) -> b p j", p=P))
                 nc.sync.dma_start(
                     out=out_rows[:, bt, dh * N_MOVE : (dh + 1) * N_MOVE], in_=result[:].rearrange("b p j -> b (p j)")
@@ -352,27 +352,40 @@ def tile_multidimensinalgrucell_pb_v_kernel(
         times_grad(2, 2, 4)
         turn_weight(2, Z_BANK)
         turn_weight(3, Z_BANK)
+        turn_v(3, [(2, 4)])
+        turn_h(3)
+        for g in range(2, 4):
+            turn_z(3, g)
+        turn_grad(3)
         quantise_dg(0, 0, GATES)
         quantise_dg(1, 0, GATES)
         for g in range(GATES):
             quantise_weight(g)
-        multiply_and_store(0)
-        multiply_and_store(1)
-        subtract_h_rows(3)
         quantise_dg(2, 0, GATES)
-        multiply_and_store(2)
-        times_z_rows(3, 0, 2)
-        times_z_rows(3, 2, 4)
+        open_sums(0)
+        open_sums(1)
+        for g in range(GATES - 1):
+            multiply(0, g, g + 1, 0, 3)
+            multiply(1, g, g + 1, 0, 3)
+        for bt in range(2):
+            multiply(bt, 3, 4, 0, 3)
+            store(bt)
+        subtract_h_rows(3, 0, 2)
+        times_z_rows(3, 0, 1)
+        times_z_rows(3, 1, 2)
+        times_grad_rows(3, 0, 2)
+        subtract_h(3, [(2, 4)])
+        times_z(3, 2, 4)
+        open_sums(2)
+        multiply(2, 0, 4, 0, 3, [0])
+        turn_dg(3, 0, 2)
+        store(2, [0])
+        multiply(2, 0, 4, 0, 3, [1])
         open_sums(3)
+        times_grad(3, 2, 3)
+        times_grad(3, 3, 4)
         for g in range(GATES):
-            times_grad_rows(3, g, g + 1)
-            if g == 3:
-                multiply(3, 0, 1, 0, 3)
-            turn_dg(3, g, g + 1)
-            if g >= 2:
-                quantise_dg(3, g - 2, g - 1)
-        quantise_dg(3, 2, 3)
-        quantise_dg(3, 3, 4)
-        for g in range(1, GATES):
-            multiply(3, g, g + 1, 0, 3)
+            quantise_dg(3, g, g + 1)
+        multiply(3, 0, 4, 0, 3)
+        store(2, [1])
         store(3)

@@ -128,10 +128,10 @@ def tile_multidimensinalgrucell_pb_v_kernel(
         acc_banks = [(S_BANK, S_BANK), (Z_BANK, Z_BANK), (S_BANK, S_BANK), (Z_BANK, Z_BANK)]
         h_banks, grad_banks, z_banks = {}, {}, {}
 
-        def turn_weight(g, bank):
+        def turn_weight(g, bank, first=0, end=D_TILES // 2):
             words = w_tiles[g][:].bitcast(F32).rearrange("p t (q c) -> p t c q", c=2)
             grouped_words = w_grouped[g][:].bitcast(F32)
-            for two in range(D_TILES // 2):
+            for two in range(first, end):
                 turned = psum.tile([P, 2, 2 * P], F32, tag=bank[0], bufs=bank[1], name="turned")
                 for j in range(2):
                     for c in range(2):
@@ -292,10 +292,10 @@ def tile_multidimensinalgrucell_pb_v_kernel(
             for tag, bufs in acc_banks[bt]:
                 acc_tiles[bt].append(psum.tile([P, N_MOVE], F32, tag=tag, bufs=bufs, name="acc"))
 
-        def multiply(bt, lo, hi, first, last, halves=range(D_HALVES)):
+        def multiply(bt, gates, first=0, last=GATES - 1, halves=range(D_HALVES)):
             for dh in halves:
                 d_cols = slice(dh * N_MOVE, (dh + 1) * N_MOVE)
-                for g in range(lo, hi):
+                for g in gates:
                     nc.tensor.matmul_mx(
                         out=acc_tiles[bt][dh][:],
                         lhsT=dg_codes[:, bt, g, :].bitcast(E5M2_X4),
@@ -316,22 +316,22 @@ def tile_multidimensinalgrucell_pb_v_kernel(
 
         def multiply_and_store(bt):
             open_sums(bt)
-            multiply(bt, 0, GATES, 0, GATES - 1)
+            multiply(bt, range(GATES))
             store(bt)
 
         gate_products(nc.vector, 0, 0, GATES)
-        for lo, hi in gate_pairs:
-            turn_v(0, [(lo, hi)])
-            turn_h(0, lo, hi)
+        turn_v(0, [(0, 2)])
+        turn_h(0)
+        turn_v(0, [(2, 4)])
         for g in range(GATES):
             turn_z(0, g)
-        turn_grad(0)
         subtract_h(0)
         gate_products(nc.gpsimd, 1, 0, GATES)
         for bt in range(2, 4):
             gate_products(nc.gpsimd, bt, 0, GATES)
         sum_products(nc.gpsimd, 3)
         turn_v(1)
+        turn_grad(0)
         turn_h(1)
         times_z(0)
         times_grad(0, 0, 2)
@@ -345,8 +345,10 @@ def tile_multidimensinalgrucell_pb_v_kernel(
         times_grad(1, 2, 4)
         turn_weight(0, S_BANK)
         turn_grad(2)
-        turn_weight(1, S_BANK)
+        turn_weight(1, S_BANK, 0, 2)
         subtract_h(2)
+        turn_weight(1, H_BANK, 2, 3)
+        turn_weight(1, S_BANK, 3, 4)
         times_z(2)
         times_grad_gpsimd(2, 0, 2)
         times_grad(2, 2, 4)
@@ -359,16 +361,17 @@ def tile_multidimensinalgrucell_pb_v_kernel(
         turn_grad(3)
         quantise_dg(0, 0, GATES)
         quantise_dg(1, 0, GATES)
-        for g in range(GATES):
+        for g in range(GATES - 1):
             quantise_weight(g)
         quantise_dg(2, 0, GATES)
+        quantise_weight(GATES - 1)
         open_sums(0)
         open_sums(1)
         for g in range(GATES - 1):
-            multiply(0, g, g + 1, 0, 3)
-            multiply(1, g, g + 1, 0, 3)
+            multiply(0, (g,))
+            multiply(1, (g,))
         for bt in range(2):
-            multiply(bt, 3, 4, 0, 3)
+            multiply(bt, (GATES - 1,))
             store(bt)
         subtract_h_rows(3, 0, 2)
         times_z_rows(3, 0, 1)
@@ -377,15 +380,15 @@ def tile_multidimensinalgrucell_pb_v_kernel(
         subtract_h(3, [(2, 4)])
         times_z(3, 2, 4)
         open_sums(2)
-        multiply(2, 0, 4, 0, 3, [0])
+        multiply(2, range(GATES), halves=(0,))
         turn_dg(3, 0, 2)
         store(2, [0])
-        multiply(2, 0, 4, 0, 3, [1])
+        multiply(2, range(GATES), halves=(1,))
         open_sums(3)
         times_grad(3, 2, 3)
         times_grad(3, 3, 4)
-        for g in range(GATES):
+        for g in (2, 3, 0, 1):
             quantise_dg(3, g, g + 1)
-        multiply(3, 0, 4, 0, 3)
+        multiply(3, (2, 3, 0, 1), first=2, last=1)
         store(2, [1])
         store(3)

@@ -76,6 +76,10 @@ def tile_multidimensinalgrucell_pb_v_kernel(
         def load_v_pair(i, g):
             nc.sync.dma_start(out=v_tiles[i][:, g, :, :], in_=blended_rows[g][:, 2 * i : 2 * i + 2, :])
 
+        def load_z_half(bt, g, half):
+            cols = slice(half * (U // 2), (half + 1) * (U // 2))
+            nc.sync.dma_start(out=z_tiles[bt][:, g, cols], in_=z_rows[:, bt, g, cols])
+
         def load_z(bt, lo, hi):
             nc.sync.dma_start(out=z_tiles[bt][:, lo:hi, :], in_=z_rows[:, bt, lo:hi, :])
 
@@ -88,9 +92,12 @@ def tile_multidimensinalgrucell_pb_v_kernel(
                 in_=weights[g][KD - D : KD, :].rearrange("(h p j) u -> p h j u", h=D_HALVES, p=P),
             )
 
-        for g in range(GATES):
+        for g in range(GATES - 1):
             load_v(0, g)
             load_z(0, g, g + 1)
+        load_v(0, 3)
+        load_z_half(0, 3, 0)
+        load_z_half(0, 3, 1)
         for lo, hi in gate_pairs:
             for g in range(lo, hi):
                 load_v(1, g)
@@ -151,6 +158,15 @@ def tile_multidimensinalgrucell_pb_v_kernel(
             )
 
         prod_tiles = {}
+
+        def half_product(bt, g, half):
+            cols = slice(half * (U // 2), (half + 1) * (U // 2))
+            nc.vector.tensor_tensor(
+                out=prod_tiles[bt][:, g, cols],
+                in0=z_tiles[bt][:, g, cols],
+                in1=v_tiles[bt // 2][:, g, bt % 2, cols],
+                op=MULT,
+            )
 
         def gate_products(engine, bt, lo, hi):
             if lo == 0:
@@ -249,7 +265,7 @@ def tile_multidimensinalgrucell_pb_v_kernel(
                 nc.vector.tensor_tensor(
                     out=diff[bt % 2][:, lo:hi, :, :],
                     in0=v_turned[bt][:, lo:hi, :, :],
-                    in1=h_banks[bt][:].rearrange("q t b -> q b t").unsqueeze(1).to_broadcast([P, 2, P, PACK]),
+                    in1=h_banks[bt][:].rearrange("q t b -> q b t").unsqueeze(1).to_broadcast([P, hi - lo, P, PACK]),
                     op=SUB,
                 )
 
@@ -309,17 +325,25 @@ def tile_multidimensinalgrucell_pb_v_kernel(
         def store(bt, halves=range(D_HALVES)):
             for dh in halves:
                 result = work.tile([P, P, TILES_PER_HALF], F32, tag="result", bufs=6)
-                nc.scalar.copy(out=result[:], in_=acc_tiles[bt][dh][:].rearrange("b (j p) -> b p j", p=P))
-                nc.sync.dma_start(
-                    out=out_rows[:, bt, dh * N_MOVE : (dh + 1) * N_MOVE], in_=result[:].rearrange("b p j -> b (p j)")
-                )
+                in_order = acc_tiles[bt][dh][:].rearrange("b (j p) -> b p j", p=P)
+                parts = 2 if (bt, dh) == (B_TILES - 1, D_HALVES - 1) else 1
+                for k in range(parts):
+                    rows = slice(k * P // parts, (k + 1) * P // parts)
+                    nc.scalar.copy(out=result[:, rows, :], in_=in_order[:, rows, :])
+                    d0 = dh * N_MOVE + k * N_MOVE // parts
+                    nc.sync.dma_start(
+                        out=out_rows[:, bt, d0 : d0 + N_MOVE // parts],
+                        in_=result[:, rows, :].rearrange("b p j -> b (p j)"),
+                    )
 
         def multiply_and_store(bt):
             open_sums(bt)
             multiply(bt, range(GATES))
             store(bt)
 
-        gate_products(nc.vector, 0, 0, GATES)
+        gate_products(nc.vector, 0, 0, 3)
+        half_product(0, 3, 0)
+        half_product(0, 3, 1)
         turn_v(0, [(0, 2)])
         turn_h(0)
         turn_v(0, [(2, 4)])
@@ -340,10 +364,14 @@ def tile_multidimensinalgrucell_pb_v_kernel(
         turn_v(2)
         subtract_h(1)
         turn_h(2)
-        times_z(1)
+        times_z(1, 0, 2)
+        turn_weight(0, S_BANK, 0, 1)
+        times_z(1, 2, 3)
+        turn_weight(0, S_BANK, 1, 2)
+        times_z(1, 3, 4)
+        turn_weight(0, S_BANK, 2, 4)
         times_grad(1, 0, 2)
         times_grad(1, 2, 4)
-        turn_weight(0, S_BANK)
         turn_grad(2)
         turn_weight(1, S_BANK, 0, 2)
         subtract_h(2)
@@ -363,6 +391,7 @@ def tile_multidimensinalgrucell_pb_v_kernel(
         quantise_dg(1, 0, GATES)
         for g in range(GATES - 1):
             quantise_weight(g)
+        subtract_h_rows(3, 0, 2)
         quantise_dg(2, 0, GATES)
         quantise_weight(GATES - 1)
         open_sums(0)
@@ -373,7 +402,6 @@ def tile_multidimensinalgrucell_pb_v_kernel(
         for bt in range(2):
             multiply(bt, (GATES - 1,))
             store(bt)
-        subtract_h_rows(3, 0, 2)
         times_z_rows(3, 0, 1)
         times_z_rows(3, 1, 2)
         times_grad_rows(3, 0, 2)

@@ -230,8 +230,6 @@ def tile_multidimensinalgrucell_pb_v_kernel(
             for c in range(2):
                 nc.tensor.transpose(bank[:, :, c], words[:, c, :], identity[:])
             grad_banks[bt] = bank
-            if bt == 2:
-                nc.scalar.copy(out=grad_turned[:].bitcast(F32), in_=bank[:])
 
         def turn_planes(bank, rows):
             planes = rows.rearrange("p (q t) -> p t q", t=PACK)
@@ -287,12 +285,6 @@ def tile_multidimensinalgrucell_pb_v_kernel(
                 in1=grad_banks[bt][:].bitcast(BF16).unsqueeze(1).to_broadcast([P, hi - lo, P, PACK]),
                 op=MULT,
             )
-
-        def times_grad_gpsimd(bt, lo, hi):
-            for g in range(lo, hi):
-                nc.gpsimd.tensor_tensor(
-                    out=dg_grouped[bt][:, g, :, :], in0=diff[bt % 2][:, g, :, :], in1=grad_turned[:], op=MULT
-                )
 
         def quantise_dg(bt, lo, hi):
             nc.vector.quantize_mx(
@@ -378,7 +370,7 @@ def tile_multidimensinalgrucell_pb_v_kernel(
         turn_weight(1, H_BANK, 2, 3)
         turn_weight(1, S_BANK, 3, 4)
         times_z(2)
-        times_grad_gpsimd(2, 0, 2)
+        times_grad(2, 0, 2)
         times_grad(2, 2, 4)
         turn_weight(2, Z_BANK)
         turn_weight(3, Z_BANK)

@@ -98,10 +98,12 @@ def tile_multidimensinalgrucell_pb_v_kernel(
         load_v(0, 3)
         load_z_half(0, 3, 0)
         load_z_half(0, 3, 1)
-        for lo, hi in gate_pairs:
-            for g in range(lo, hi):
-                load_v(1, g)
-            load_z(1, lo, hi)
+        for g in range(2):
+            load_v(1, g)
+            load_z(1, g, g + 1)
+        for g in range(2, GATES):
+            load_v(1, g)
+        load_z(1, 2, GATES)
         load_grad(0)
         for lo, hi in gate_pairs:
             for g in range(lo, hi):
@@ -168,14 +170,14 @@ def tile_multidimensinalgrucell_pb_v_kernel(
                 op=MULT,
             )
 
-        def gate_products(engine, bt, lo, hi):
-            if lo == 0:
+        def gate_products(engine, bt, groups):
+            if groups[0][0] == 0:
                 prod_tiles[bt] = work.tile([P, GATES, U], F32, tag="prod", name="prod", bufs=3)
-            for g in range(lo, hi):
+            for lo, hi in groups:
                 engine.tensor_tensor(
-                    out=prod_tiles[bt][:, g, :],
-                    in0=z_tiles[bt][:, g, :],
-                    in1=v_tiles[bt // 2][:, g, bt % 2, :],
+                    out=prod_tiles[bt][:, lo:hi, :],
+                    in0=z_tiles[bt][:, lo:hi, :],
+                    in1=v_tiles[bt // 2][:, lo:hi, bt % 2, :],
                     op=MULT,
                 )
 
@@ -222,7 +224,9 @@ def tile_multidimensinalgrucell_pb_v_kernel(
                 for g in range(lo, hi):
                     for c in range(2):
                         nc.tensor.transpose(turned[:, g - lo, c, :], words[:, g, c, :], identity[:])
-                nc.scalar.copy(out=turned_words[:, lo:hi, :, :], in_=turned[:].rearrange("q g c b -> q g b c"))
+                nc.scalar.copy(
+                    out=turned_words[:, lo:hi, :, :], in_=turned[:, 0 : hi - lo, :, :].rearrange("q g c b -> q g b c")
+                )
 
         def turn_grad(bt):
             words = grad_tiles[bt // 2][:].bitcast(F32)[:, bt % 2, :].rearrange("p (q c) -> p c q", c=2)
@@ -333,18 +337,19 @@ def tile_multidimensinalgrucell_pb_v_kernel(
             multiply(bt, range(GATES))
             store(bt)
 
-        gate_products(nc.vector, 0, 0, 3)
+        gate_products(nc.vector, 0, [(g, g + 1) for g in range(3)])
         half_product(0, 3, 0)
         half_product(0, 3, 1)
         turn_v(0, [(0, 2)])
         turn_h(0)
-        turn_v(0, [(2, 4)])
+        turn_v(0, [(2, 3), (3, 4)])
         for g in range(GATES):
             turn_z(0, g)
-        subtract_h(0)
-        gate_products(nc.gpsimd, 1, 0, GATES)
+        gate_products(nc.vector, 1, [(0, 1)])
+        subtract_h(0, [(0, 2), (2, 3), (3, 4)])
+        gate_products(nc.gpsimd, 1, [(g, g + 1) for g in range(1, GATES)])
         for bt in range(2, 4):
-            gate_products(nc.gpsimd, bt, 0, GATES)
+            gate_products(nc.gpsimd, bt, gate_pairs)
         sum_products(nc.gpsimd, 3)
         turn_v(1)
         turn_grad(0)

from contextlib import ExitStack

import concourse.mybir as mybir
from concourse.masks import make_identity

F32 = mybir.dt.float32
BF16 = mybir.dt.bfloat16
U32 = mybir.dt.uint32
U8 = mybir.dt.uint8
E4M3_X4 = mybir.dt.float8_e4m3fn_x4
E5M2_X4 = mybir.dt.float8_e5m2_x4
ADD = mybir.AluOpType.add
SUB = mybir.AluOpType.subtract
MULT = mybir.AluOpType.mult

P = 128
PACK = 4
B, D, U = 512, 1024, 512
GATES = 4
KD = 3 * U + D
B_TILES = B // P
D_TILES = D // P
N_MOVE = 512
D_HALVES = D // N_MOVE
TILES_PER_HALF = N_MOVE // P

FLOPS = 2 * B * D * GATES * U
BYTES = 4 * B * GATES * U + 2 * 5 * B * U + 2 * GATES * D * U + 4 * B * D


def tile_multidimensinalgrucell_pb_v_kernel(
    tc,
    x,
    left_state,
    top_state,
    diagonal_state,
    h_cand,
    w_zi,
    b_zi,
    w_zl,
    b_zl,
    w_zt,
    b_zt,
    w_zd,
    b_zd,
    z,
    grad_out,
    out,
):
    nc = tc.nc
    blended = [h_cand, left_state, top_state, diagonal_state]
    weights = [w_zi, w_zl, w_zt, w_zd]

    z_rows = z.rearrange("(p t) (g u) -> p t g u", t=B_TILES, g=GATES)
    blended_rows = [v.rearrange("(p t) u -> p t u", t=B_TILES) for v in blended]
    grad_rows = grad_out.rearrange("(p t) u -> p t u", t=B_TILES)
    out_rows = out.rearrange("(p t) d -> p t d", t=B_TILES)

    with ExitStack() as ctx:
        ctx.enter_context(tc.manual_schedule())
        inputs = ctx.enter_context(tc.tile_pool(name="inputs", bufs=1))
        keep = ctx.enter_context(tc.tile_pool(name="keep", bufs=1))
        work = ctx.enter_context(tc.tile_pool(name="work", bufs=2))
        psum = ctx.enter_context(tc.psum_pool(name="psum", bufs=2))

        gate_pairs = [(0, 2), (2, 4)]

        z_tiles = [inputs.tile([P, GATES, U], F32, name="z%d" % bt) for bt in range(B_TILES)]
        v_tiles = [inputs.tile([P, GATES, 2, U], BF16, name="v%d" % i) for i in range(B_TILES // 2)]
        grad_tiles = [inputs.tile([P, 2, U], BF16, name="grad%d" % i) for i in range(B_TILES // 2)]
        w_tiles = [inputs.tile([P, D_TILES, U], BF16, name="w%d" % g) for g in range(GATES)]

        def load_v(bt, g):
            nc.sync.dma_start(out=v_tiles[bt // 2][:, g, bt % 2, :], in_=blended_rows[g][:, bt, :])

        def load_v_pair(i, g):
            nc.sync.dma_start(out=v_tiles[i][:, g, :, :], in_=blended_rows[g][:, 2 * i : 2 * i + 2, :])

        def load_z_half(bt, g, half):
            cols = slice(half * (U // 2), (half + 1) * (U // 2))
            nc.sync.dma_start(out=z_tiles[bt][:, g, cols], in_=z_rows[:, bt, g, cols])

        def load_z(bt, lo, hi):
            nc.sync.dma_start(out=z_tiles[bt][:, lo:hi, :], in_=z_rows[:, bt, lo:hi, :])

        def load_grad(i):
            nc.sync.dma_start(out=grad_tiles[i][:], in_=grad_rows[:, 2 * i : 2 * i + 2, :])

        def load_weight(g):
            nc.sync.dma_start(
                out=w_tiles[g][:].rearrange("p (h j) u -> p h j u", h=D_HALVES),
                in_=weights[g][KD - D : KD, :].rearrange("(h p j) u -> p h j u", h=D_HALVES, p=P),
            )

        for g in range(GATES - 1):
            load_v(0, g)
            load_z(0, g, g + 1)
        load_v(0, 3)
        load_z_half(0, 3, 0)
        load_z_half(0, 3, 1)
        for g in range(2):
            load_v(1, g)
            load_z(1, g, g + 1)
        for g in range(2, GATES):
            load_v(1, g)
        load_z(1, 2, GATES)
        load_grad(0)
        for lo, hi in gate_pairs:
            for g in range(lo, hi):
                load_v_pair(1, g)
            load_z(2, lo, hi)
        load_grad(1)
        for lo, hi in gate_pairs:
            load_z(3, lo, hi)
        for g in range(GATES):
            load_weight(g)

        identity = keep.tile([P, P], F32, name="identity")
        make_identity(nc, identity[:])

        w_codes = keep.tile([P, GATES, D], U32, name="w_codes", align_bytes=64)
        w_scales = keep.tile([P, GATES, D], U8, name="w_scales", align_bytes=64)
        dg_codes = keep.tile([P, B_TILES, GATES, P], U32, name="dg_codes", align_bytes=64)
        dg_scales = keep.tile([P, B_TILES, GATES, P], U8, name="dg_scales", align_bytes=64)
        w_grouped = [
            keep.tile([P, D, PACK], BF16, name="w_grouped%d" % g, align_bytes=64) for g in range(GATES)
        ]
        dg_grouped = [
            keep.tile([P, GATES, P, PACK], BF16, name="dg_grouped%d" % i, align_bytes=64) for i in range(B_TILES)
        ]
        h_rows = keep.tile([P, U], F32, name="h_rows")
        dg_rows = keep.tile([P, 2, U], BF16, name="dg_rows")
        grad_turned = keep.tile([P, P, PACK], BF16, name="grad_turned")
        v_turned = [keep.tile([P, GATES, P, PACK], BF16, name="v_turned%d" % bt) for bt in range(B_TILES)]
        diff = [keep.tile([P, GATES, P, PACK], F32, name="diff%d" % i) for i in range(2)]
        H_BANK, G_BANK, Z_BANK, S_BANK = ("h_bank", 1), ("grad_bank", 1), ("z_bank", GATES), ("stage", 2)
        acc_banks = [(S_BANK, S_BANK), (Z_BANK, Z_BANK), (S_BANK, S_BANK), (Z_BANK, Z_BANK)]
        h_banks, grad_banks, z_banks = {}, {}, {}

        def turn_weight(g, bank, first=0, end=D_TILES // 2):
            words = w_tiles[g][:].bitcast(F32).rearrange("p t (q c) -> p t c q", c=2)
            grouped_words = w_grouped[g][:].bitcast(F32)
            for two in range(first, end):
                turned = psum.tile([P, 2, 2 * P], F32, tag=bank[0], bufs=bank[1], name="turned")
                for j in range(2):
                    for c in range(2):
                        nc.tensor.transpose(
                            turned[:, c, j * P : (j + 1) * P], words[:, 2 * two + j, c, :], identity[:]
                        )
                nc.scalar.copy(
                    out=grouped_words[:, 2 * two * P : (2 * two + 2) * P, :],
                    in_=turned[:].rearrange("q c d -> q d c"),
                )

        def quantise_weight(g):
            nc.vector.quantize_mx(
                out=w_codes[:, g, :].bitcast(E4M3_X4),
                scales=w_scales[:, g, :],
                in_=w_grouped[g][:].rearrange("q d t -> q (d t)"),
            )

        prod_tiles = {}

        def half_product(bt, g, half):
            cols = slice(half * (U // 2), (half + 1) * (U // 2))
            nc.vector.tensor_tensor(
                out=prod_tiles[bt][:, g, cols],
                in0=z_tiles[bt][:, g, cols],
                in1=v_tiles[bt // 2][:, g, bt % 2, cols],
                op=MULT,
            )

        def gate_products(engine, bt, groups):
            if groups[0][0] == 0:
                prod_tiles[bt] = work.tile([P, GATES, U], F32, tag="prod", name="prod", bufs=3)
            for lo, hi in groups:
                engine.tensor_tensor(
                    out=prod_tiles[bt][:, lo:hi, :],
                    in0=z_tiles[bt][:, lo:hi, :],
                    in1=v_tiles[bt // 2][:, lo:hi, bt % 2, :],
                    op=MULT,
                )

        def sum_products(engine, bt):
            prod = prod_tiles[bt]
            engine.tensor_tensor(out=prod[:, 0:2, :], in0=prod[:, 0:2, :], in1=prod[:, 2:4, :], op=ADD)
            engine.tensor_tensor(out=h_rows[:], in0=prod[:, 0, :], in1=prod[:, 1, :], op=ADD)

        def subtract_h_rows(bt, lo, hi):
            nc.vector.tensor_tensor(
                out=diff[bt % 2][:].rearrange("p g b t -> p g (b t)")[:, lo:hi, :],
                in0=v_tiles[bt // 2][:, lo:hi, bt % 2, :],
                in1=h_rows[:].unsqueeze(1).to_broadcast([P, hi - lo, U]),
                op=SUB,
            )

        def times_z_rows(bt, lo, hi):
            rows = diff[bt % 2][:].rearrange("p g b t -> p g (b t)")[:, lo:hi, :]
            nc.vector.tensor_tensor(out=rows, in0=rows, in1=z_tiles[bt][:, lo:hi, :], op=MULT)

        def times_grad_rows(bt, lo, hi):
            rows = diff[bt % 2][:].rearrange("p g b t -> p g (b t)")
            for g in range(lo, hi):
                nc.gpsimd.tensor_tensor(
                    out=dg_rows[:, g, :], in0=rows[:, g, :], in1=grad_tiles[bt // 2][:, bt % 2, :], op=MULT
                )

        def turn_dg(bt, lo, hi):
            words = dg_rows[:].bitcast(F32).rearrange("p g (q c) -> p g c q", c=2)
            turned = psum.tile([P, 2, 2, P], F32, tag="h_bank", bufs=1, name="turned_dg")
            for g in range(lo, hi):
                for c in range(2):
                    nc.tensor.transpose(turned[:, g - lo, c, :], words[:, g, c, :], identity[:])
            nc.scalar.copy(
                out=dg_grouped[bt][:].bitcast(F32)[:, lo:hi, :, :],
                in_=turned[:, 0 : hi - lo, :, :].rearrange("q g c b -> q g b c"),
            )

        def turn_v(bt, pairs=gate_pairs):
            words = v_tiles[bt // 2][:].bitcast(F32)[:, :, bt % 2, :].rearrange("p g (q c) -> p g c q", c=2)
            turned_words = v_turned[bt][:].bitcast(F32)
            for lo, hi in pairs:
                turned = psum.tile([P, 2, 2, P], F32, tag="stage")
                for g in range(lo, hi):
                    for c in range(2):
                        nc.tensor.transpose(turned[:, g - lo, c, :], words[:, g, c, :], identity[:])
                nc.scalar.copy(
                    out=turned_words[:, lo:hi, :, :], in_=turned[:, 0 : hi - lo, :, :].rearrange("q g c b -> q g b c")
                )

        def turn_grad(bt):
            words = grad_tiles[bt // 2][:].bitcast(F32)[:, bt % 2, :].rearrange("p (q c) -> p c q", c=2)
            bank = psum.tile([P, P, 2], F32, tag="grad_bank", bufs=1)
            for c in range(2):
                nc.tensor.transpose(bank[:, :, c], words[:, c, :], identity[:])
            grad_banks[bt] = bank

        def turn_planes(bank, rows):
            planes = rows.rearrange("p (q t) -> p t q", t=PACK)
            for t in range(PACK):
                nc.tensor.transpose(bank[:, t, :], planes[:, t, :], identity[:])

        def turn_h(bt, lo=0, hi=GATES):
            if lo == 0:
                h_banks[bt] = psum.tile([P, PACK, P], F32, tag="h_bank", bufs=1, name="h_bank")
            if bt == 3:
                turn_planes(h_banks[bt], h_rows[:])
                return
            for g in range(lo, hi):
                planes = prod_tiles[bt][:, g, :].rearrange("p (q t) -> p t q", t=PACK)
                for t in range(PACK):
                    nc.tensor.matmul(
                        out=h_banks[bt][:, t, :],
                        lhsT=planes[:, t, :],
                        rhs=identity[:],
                        is_transpose=True,
                        start=(g == 0 and t == 0),
                        stop=(g == GATES - 1 and t == PACK - 1),
                    )

        def turn_z(bt, g):
            z_banks[(bt, g)] = psum.tile([P, PACK, P], F32, tag="z_bank", bufs=GATES, name="z_bank")
            turn_planes(z_banks[(bt, g)], z_tiles[bt][:, g, :])

        def subtract_h(bt, pairs=gate_pairs):
            for lo, hi in pairs:
                nc.vector.tensor_tensor(
                    out=diff[bt % 2][:, lo:hi, :, :],
                    in0=v_turned[bt][:, lo:hi, :, :],
                    in1=h_banks[bt][:].rearrange("q t b -> q b t").unsqueeze(1).to_broadcast([P, hi - lo, P, PACK]),
                    op=SUB,
                )

        def times_z(bt, lo=0, hi=GATES):
            for g in range(lo, hi):
                nc.vector.tensor_tensor(
                    out=diff[bt % 2][:, g, :, :],
                    in0=diff[bt % 2][:, g, :, :],
                    in1=z_banks[(bt, g)][:].rearrange("q t b -> q b t"),
                    op=MULT,
                )
                if bt + 1 < 3:
                    turn_z(bt + 1, g)

        def times_grad(bt, lo, hi):
            nc.vector.tensor_tensor(
                out=dg_grouped[bt][:, lo:hi, :, :],
                in0=diff[bt % 2][:, lo:hi, :, :],
                in1=grad_banks[bt][:].bitcast(BF16).unsqueeze(1).to_broadcast([P, hi - lo, P, PACK]),
                op=MULT,
            )

        def quantise_dg(bt, lo, hi):
            nc.vector.quantize_mx(
                out=dg_codes[:, bt, lo:hi, :].rearrange("q g b -> q (g b)").bitcast(E5M2_X4),
                scales=dg_scales[:, bt, lo:hi, :].rearrange("q g b -> q (g b)"),
                in_=dg_grouped[bt][:, lo:hi, :, :].rearrange("q g b t -> q (g b t)"),
            )

        acc_tiles = {}

        def open_sums(bt):
            acc_tiles[bt] = []
            for tag, bufs in acc_banks[bt]:
                acc_tiles[bt].append(psum.tile([P, N_MOVE], F32, tag=tag, bufs=bufs, name="acc"))

        def multiply(bt, gates, first=0, last=GATES - 1, halves=range(D_HALVES)):
            for dh in halves:
                d_cols = slice(dh * N_MOVE, (dh + 1) * N_MOVE)
                for g in gates:
                    nc.tensor.matmul_mx(
                        out=acc_tiles[bt][dh][:],
                        lhsT=dg_codes[:, bt, g, :].bitcast(E5M2_X4),
                        lhsT_scale=dg_scales[:, bt, g, :],
                        rhs=w_codes[:, g, d_cols].bitcast(E4M3_X4),
                        rhs_scale=w_scales[:, g, d_cols],
                        start=(g == first),
                        stop=(g == last),
                    )

        def store(bt, halves=range(D_HALVES)):
            for dh in halves:
                result = work.tile([P, P, TILES_PER_HALF], F32, tag="result", bufs=6)
                in_order = acc_tiles[bt][dh][:].rearrange("b (j p) -> b p j", p=P)
                parts = 2 if (bt, dh) == (B_TILES - 1, D_HALVES - 1) else 1
                for k in range(parts):
                    rows = slice(k * P // parts, (k + 1) * P // parts)
                    nc.scalar.copy(out=result[:, rows, :], in_=in_order[:, rows, :])
                    d0 = dh * N_MOVE + k * N_MOVE // parts
                    nc.sync.dma_start(
                        out=out_rows[:, bt, d0 : d0 + N_MOVE // parts],
                        in_=result[:, rows, :].rearrange("b p j -> b (p j)"),
                    )

        def multiply_and_store(bt):
            open_sums(bt)
            multiply(bt, range(GATES))
            store(bt)

        gate_products(nc.vector, 0, [(g, g + 1) for g in range(3)])
        half_product(0, 3, 0)
        half_product(0, 3, 1)
        turn_v(0, [(0, 2)])
        turn_h(0)
        turn_v(0, [(2, 3), (3, 4)])
        for g in range(GATES):
            turn_z(0, g)
        gate_products(nc.vector, 1, [(0, 1)])
        subtract_h(0, [(0, 2), (2, 3), (3, 4)])
        gate_products(nc.gpsimd, 1, [(g, g + 1) for g in range(1, GATES)])
        for bt in range(2, 4):
            gate_products(nc.gpsimd, bt, gate_pairs)
        sum_products(nc.gpsimd, 3)
        turn_v(1)
        turn_grad(0)
        turn_h(1)
        times_z(0)
        times_grad(0, 0, 2)
        times_grad(0, 2, 4)
        turn_grad(1)
        turn_v(2)
        subtract_h(1)
        turn_h(2)
        times_z(1, 0, 2)
        turn_weight(0, S_BANK, 0, 1)
        times_z(1, 2, 3)
        turn_weight(0, S_BANK, 1, 2)
        times_z(1, 3, 4)
        turn_weight(0, S_BANK, 2, 4)
        times_grad(1, 0, 2)
        times_grad(1, 2, 4)
        turn_grad(2)
        turn_weight(1, S_BANK, 0, 2)
        subtract_h(2)
        turn_weight(1, H_BANK, 2, 3)
        turn_weight(1, S_BANK, 3, 4)
        times_z(2)
        times_grad(2, 0, 2)
        times_grad(2, 2, 4)
        turn_weight(2, Z_BANK)
        turn_weight(3, Z_BANK)
        turn_v(3, [(2, 4)])
        turn_h(3)
        for g in range(2, 4):
            turn_z(3, g)
        turn_grad(3)
        quantise_dg(0, 0, GATES)
        quantise_dg(1, 0, GATES)
        for g in range(GATES - 1):
            quantise_weight(g)
        subtract_h_rows(3, 0, 2)
        quantise_dg(2, 0, GATES)
        quantise_weight(GATES - 1)
        open_sums(0)
        open_sums(1)
        for g in range(GATES - 1):
            multiply(0, (g,))
            multiply(1, (g,))
        for bt in range(2):
            multiply(bt, (GATES - 1,))
            store(bt)
        times_z_rows(3, 0, 1)
        times_z_rows(3, 1, 2)
        times_grad_rows(3, 0, 2)
        subtract_h(3, [(2, 4)])
        times_z(3, 2, 4)
        open_sums(2)
        multiply(2, range(GATES), halves=(0,))
        turn_dg(3, 0, 2)
        store(2, [0])
        multiply(2, range(GATES), halves=(1,))
        open_sums(3)
        times_grad(3, 2, 3)
        times_grad(3, 3, 4)
        for g in (2, 3, 0, 1):
            quantise_dg(3, g, g + 1)
        multiply(3, (2, 3, 0, 1), first=2, last=1)
        store(2, [1])
        store(3)
